import numpy as np
import ml_dtypes


def mxq(x, axis, fmt="e4m3"):
    dtype, down = {"e4m3": (ml_dtypes.float8_e4m3fn, 7), "e5m2": (ml_dtypes.float8_e5m2, 14)}[fmt]
    v = np.moveaxis(np.asarray(x, np.float32).astype(ml_dtypes.bfloat16).astype(np.float64), axis, -1)
    blocks = v.reshape(v.shape[:-1] + (-1, 32))
    amax = np.abs(blocks).max(-1, keepdims=True)
    byte = np.maximum(np.where(amax > 0, np.frexp(amax)[1] - 1 + 127, 0) - down, 1)
    scale = np.exp2(byte - 127.0)
    codes = (blocks / scale).astype(np.float32).astype(dtype).astype(np.float64)
    return np.moveaxis((codes * scale).reshape(v.shape), -1, axis)


WIDE = False


def mx_kscale(k):
    if not WIDE:
        return np.ones(k)
    levels = np.array([10, -10, 5, -5, 0])
    if k % 512:
        return np.exp2(np.random.permutation(np.resize(levels, k // 32))).repeat(32)
    a = np.empty((k // 512, 16))
    for p in range(k // 512):
        a[p, :8] = np.random.permutation(np.resize(levels, 8))
        for g in range(8):
            far = levels[np.abs(levels - a[p, g]) >= 10]
            a[p, g + 8] = far[np.random.randint(len(far))]
    return np.exp2(a.ravel()).repeat(32)


BF16 = ml_dtypes.bfloat16


def bf(x):
    return np.asarray(x, np.float32).astype(BF16)


def f64(x):
    return np.asarray(x).astype(np.float64)


B, N, DIM, H, DH = 2, 2048, 1024, 4, 96
D1 = DH // 3


def rotate_half(t):
    d = t.shape[-1]
    t1, t2 = t[..., : (d + 1) // 2], t[..., (d + 1) // 2:]
    return np.concatenate((-t2, t1), axis=-1)


def apply_rope(t, freqs):
    return t * np.cos(freqs) + rotate_half(t) * np.sin(freqs)


def rope3(t, fs):
    return np.concatenate([apply_rope(ts, f) for ts, f in zip(np.split(t, (D1, 2 * D1), axis=-1), fs)], axis=-1)


def setup_inputs():
    s = mx_kscale(DIM)
    return {"x": bf(np.random.standard_normal((B, N, DIM)) * s),
            "f1": bf(np.random.uniform(0.0, 1.0, (N, D1))),
            "f2": bf(np.random.uniform(0.0, 1.0, (N, D1))),
            "f3": bf(np.random.uniform(0.0, 1.0, (N, D1))),
            "Wqkv": bf(np.random.standard_normal((DIM, 3 * H * DH)) / np.sqrt(DIM) / s[:, None])}


def reference(x, f1, f2, f3, Wqkv):
    qkv = mxq(f64(x), 2, "e4m3") @ mxq(f64(Wqkv), 0, "e4m3")
    q, k, v = np.split(qkv, 3, axis=-1)
    to_heads = lambda t: t.reshape(B, N, H, DH).transpose(0, 2, 1, 3)
    q, k, v = to_heads(q), to_heads(k), to_heads(v)
    fs = (f64(f1), f64(f2), f64(f3))
    return rope3(q, fs), rope3(k, fs), v

@@ -1,0 +1,242 @@
+import math
+from contextlib import ExitStack
+
+import concourse.mybir as mybir
+from concourse.masks import make_identity
+
+F32 = mybir.dt.float32
+BF16 = mybir.dt.bfloat16
+U32 = mybir.dt.uint32
+U8 = mybir.dt.uint8
+FP8X4 = mybir.dt.float8_e4m3fn_x4
+MULT = mybir.AluOpType.mult
+ADD = mybir.AluOpType.add
+SIN = mybir.ActivationFunctionType.Sin
+
+BATCH = 2
+TOKENS = 2048
+DIM = 1024
+HEADS = 4
+HEAD_DIM = 96
+AXES = 3
+AXIS_DIM = HEAD_DIM // AXES
+HALF = AXIS_DIM // 2
+
+P = 128
+PACK = 4
+K_PASS = P * PACK
+PASSES = DIM // K_PASS
+BLOCK = HEADS * HEAD_DIM
+COLS = 3 * BLOCK
+PARTS = ((0, 256), (256, 128))
+BANK = 512
+
+TILES = TOKENS // P
+PAIR = 2
+PAIRS = BATCH * TILES // PAIR
+GROUP = 4
+VECTOR_ADDS_EVERY = 8
+
+FLOPS = 2 * BATCH * TOKENS * DIM * COLS
+
+
+def tile_attention_pa_t_kernel(tc, x, f1, f2, f3, Wqkv, out_0, out_1, out_2):
+    nc = tc.nc
+    outs = (out_0, out_1, out_2)
+
+    with ExitStack() as ctx:
+        const = ctx.enter_context(tc.tile_pool(name="const", bufs=1))
+        x_pool = ctx.enter_context(tc.tile_pool(name="x", bufs=PAIRS))
+        work = ctx.enter_context(tc.tile_pool(name="work", bufs=3))
+        psum = ctx.enter_context(tc.psum_pool(name="psum", bufs=2))
+        ctx.enter_context(tc.manual_schedule())
+
+        def load_x_pair(i):
+            b, t = divmod(i * PAIR, TILES)
+            x_pair = x_pool.tile([P, PAIR, DIM], BF16)
+            by_partition = x[b].rearrange("(p t) k -> p t k", t=TILES)
+            nc.sync.dma_start(out=x_pair[:], in_=by_partition[:, t : t + PAIR, :])
+            return x_pair
+
+        w_rows = const.tile([P, PASSES * PACK, COLS], BF16)
+        for g in range(PASSES):
+            by_partition = Wqkv[K_PASS * g : K_PASS * (g + 1), :].rearrange(
+                "(p t) c -> p t c", t=PACK
+            )
+            for u in range(2):
+                nc.sync.dma_start(
+                    out=w_rows[:, PACK * g + 2 * u : PACK * g + 2 * u + 2, :],
+                    in_=by_partition[:, 2 * u : 2 * u + 2, :],
+                )
+
+        x_pairs = [load_x_pair(0)]
+
+        angles = const.tile([P, AXES, TILES, AXIS_DIM], BF16)
+        for axis, f in enumerate((f1, f2, f3)):
+            nc.sync.dma_start(out=angles[:, axis], in_=f.rearrange("(p t) j -> p t j", t=TILES))
+
+        for i in range(1, PAIRS):
+            x_pairs.append(load_x_pair(i))
+
+        factors = const.tile([P, TILES, 2, HEAD_DIM], F32)
+
+        def make_factors(group):
+            tiles = slice(GROUP * group, GROUP * (group + 1))
+            angle = angles[:, :, tiles, :].rearrange("p a t j -> p t a j")
+            own = factors[:, tiles, 0, :].rearrange("p t (a j) -> p t a j", a=AXES)
+            partner = factors[:, tiles, 1, :].rearrange("p t (a j) -> p t a j", a=AXES)
+            nc.scalar.activation(out=own, in_=angle, func=SIN, bias=math.pi / 2, scale=-1.0)
+            nc.scalar.activation(out=partner[:, :, :, :HALF], in_=angle[:, :, :, HALF:], func=SIN)
+            nc.scalar.activation(
+                out=partner[:, :, :, HALF:], in_=angle[:, :, :, :HALF], func=SIN, scale=-1.0
+            )
+
+        warm = const.tile([P, 1], F32)
+        nc.vector.memset(warm[:], 0.0)
+        nc.scalar.activation(out=warm[:], in_=warm[:], func=SIN)
+
+        ident = const.tile([P, P], F32)
+        make_identity(nc, ident[:])
+
+        def transpose_pair(i):
+            grouped = work.tile([P, PAIR, PASSES, P, PACK], BF16, align_bytes=64)
+            for a in range(PAIR):
+                words = x_pairs[i][:, a, :].bitcast(F32)
+                xt = psum.tile([P, PASSES * 2, P], F32)
+                for g in range(PASSES):
+                    for u in range(2):
+                        first = 2 * P * g + u
+                        nc.tensor.transpose(
+                            xt[:, 2 * g + u, :], words[:, first : first + 2 * P - 1 : 2], ident[:]
+                        )
+                nc.scalar.copy(
+                    out=grouped[:, a].bitcast(F32),
+                    in_=xt[:].rearrange("p (g u) r -> p g r u", u=2),
+                )
+            return grouped
+
+        def quantise_pair(grouped):
+            x_codes = work.tile([P, PAIR, PASSES, P], U32, align_bytes=64)
+            x_scales = work.tile([P, PAIR, PASSES, P], U8, align_bytes=64)
+            nc.vector.quantize_mx(
+                out=x_codes[:].rearrange("p a g r -> p (a g r)").bitcast(FP8X4),
+                scales=x_scales[:].rearrange("p a g r -> p (a g r)"),
+                in_=grouped[:].rearrange("p a g r t -> p (a g r t)"),
+            )
+            return x_codes, x_scales
+
+
+        w_grouped = const.tile([P, PASSES, COLS, PACK], BF16, align_bytes=64)
+        w_codes = const.tile([P, PASSES, COLS], U32, align_bytes=64)
+        w_scales = const.tile([P, PASSES, COLS], U8, align_bytes=64)
+
+        def regroup_views(g, s, part):
+            c0, width = part
+            cols = slice(BLOCK * s + c0, BLOCK * s + c0 + width)
+            rows = w_rows[:, PACK * g : PACK * (g + 1), cols]
+            return (
+                w_grouped[:, g, cols, :].rearrange("p (c i) t -> p c t i", i=4),
+                rows.rearrange("p t (c i) -> p c t i", i=4),
+            )
+
+        def regroup_w(g, s):
+            wide_out, wide_in = regroup_views(g, s, PARTS[0])
+            nc.vector.tensor_copy(out=wide_out, in_=wide_in)
+            narrow_out, narrow_in = regroup_views(g, s, PARTS[1])
+            nc.scalar.copy(out=narrow_out, in_=narrow_in)
+
+        def quantise_w(g, s):
+            for c0, width in PARTS:
+                cols = slice(BLOCK * s + c0, BLOCK * s + c0 + width)
+                nc.vector.quantize_mx(
+                    out=w_codes[:, g, cols].bitcast(FP8X4),
+                    scales=w_scales[:, g, cols],
+                    in_=w_grouped[:, g, cols, :].rearrange("p c t -> p (c t)"),
+                )
+
+        pieces = [(g, s) for g in range(PASSES) for s in range(3)]
+        for n, (g, s) in enumerate(pieces):
+            regroup_w(g, s)
+            if n > 0:
+                quantise_w(*pieces[n - 1])
+        quantise_w(*pieces[-1])
+        ready = quantise_pair(transpose_pair(0))
+        make_factors(0)
+
+        def project(x_codes, x_scales, a):
+            ps_q = psum.tile([P, BANK], F32)
+            ps_k = psum.tile([P, BANK], F32)
+            ps_v = psum.tile([P, BANK], F32)
+            for s, bank in enumerate((ps_q, ps_k, ps_v)):
+                for c0, width in PARTS:
+                    cols = slice(BLOCK * s + c0, BLOCK * s + c0 + width)
+                    for g in range(PASSES):
+                        nc.tensor.matmul_mx(
+                            out=bank[:, c0 : c0 + width],
+                            lhsT=x_codes[:, a, g, :].bitcast(FP8X4),
+                            lhsT_scale=x_scales[:, a, g, :],
+                            rhs=w_codes[:, g, cols].bitcast(FP8X4),
+                            rhs_scale=w_scales[:, g, cols],
+                            start=(g == 0),
+                            stop=(g == PASSES - 1),
+                        )
+            return ps_q, ps_k, ps_v
+
+        def rope_and_collect(banks, t, staged, slot):
+            ps_q, ps_k, ps_v = banks
+            products = work.tile([P, 2, 2, BLOCK], F32)
+            shape = [P, 2, HEADS, HEAD_DIM]
+            for s, bank in enumerate((ps_q, ps_k)):
+                by_head = bank[:, :BLOCK].rearrange("p (h d) -> p h d", h=HEADS)
+                nc.vector.tensor_tensor(
+                    out=products[:, :, s, :].rearrange("p c (h d) -> p c h d", h=HEADS),
+                    in0=by_head.unsqueeze(1).to_broadcast(shape),
+                    in1=factors[:, t].unsqueeze(2).to_broadcast(shape),
+                    op=MULT,
+                )
+            split = "p s (h a f j) -> p (s h) a f j"
+            own_part = products[:, 0].rearrange(split, h=HEADS, a=AXES, f=2)
+            partner_part = products[:, 1].rearrange(split, h=HEADS, a=AXES, f=2)
+            rotated = staged[:, 0:2, :, slot, :].rearrange(
+                "p s h (a f j) -> p (s h) a f j", a=AXES, f=2
+            )
+            adder = nc.vector if t % VECTOR_ADDS_EVERY == VECTOR_ADDS_EVERY - 1 else nc.gpsimd
+            for f in range(2):
+                adder.tensor_tensor(
+                    out=rotated[:, :, :, f, :],
+                    in0=own_part[:, :, :, f, :],
+                    in1=partner_part[:, :, :, 1 - f, :],
+                    op=ADD,
+                )
+            nc.scalar.copy(
+                out=staged[:, 2, :, slot, :],
+                in_=ps_v[:, :BLOCK].rearrange("p (h d) -> p h d", h=HEADS),
+            )
+
+        def store(b, t0, count, staged, slot0):
+            for s, out in enumerate(outs):
+                by_partition = out[b].rearrange("h (p t) d -> p h t d", t=TILES)
+                nc.sync.dma_start(
+                    out=by_partition[:, :, t0 : t0 + count, :],
+                    in_=staged[:, s, :, slot0 : slot0 + count, :],
+                )
+
+        staged = None
+        for i in range(PAIRS):
+            x_codes, x_scales = ready
+            b, t0 = divmod(i * PAIR, TILES)
+            slot0 = t0 % GROUP
+            if slot0 == 0:
+                staged = work.tile([P, 3, HEADS, GROUP, HEAD_DIM], F32)
+                next_group = t0 // GROUP + 1
+                if b == 0 and next_group < TILES // GROUP:
+                    make_factors(next_group)
+            grouped = transpose_pair(i + 1) if i + 1 < PAIRS else None
+            rope_and_collect(project(x_codes, x_scales, 0), t0, staged, slot0)
+            if grouped is not None:
+                ready = quantise_pair(grouped)
+            rope_and_collect(project(x_codes, x_scales, 1), t0 + 1, staged, slot0 + 1)
+            if i * PAIR >= BATCH * TILES - GROUP:
+                store(b, t0, PAIR, staged, slot0)
+            elif slot0 + PAIR == GROUP:
+                store(b, t0 + PAIR - GROUP, GROUP, staged, 0)

@@ -18,9 +18,10 @@ TOKENS = 2048
 DIM = 1024
 HEADS = 4
 HEAD_DIM = 96
-AXES = 3
-AXIS_DIM = HEAD_DIM // AXES
+AXIS_DIM = 32
 HALF = AXIS_DIM // 2
+LATE_DIM = HEAD_DIM - AXIS_DIM
+QK_HEADS = 2 * HEADS
 
 P = 128
 PACK = 4
@@ -28,14 +29,15 @@ K_PASS = P * PACK
 PASSES = DIM // K_PASS
 BLOCK = HEADS * HEAD_DIM
 COLS = 3 * BLOCK
-PARTS = ((0, 256), (256, 128))
+AXIS0 = slice(0, QK_HEADS * AXIS_DIM)
+LATE = slice(AXIS0.stop, AXIS0.stop + QK_HEADS * LATE_DIM)
+V_PARTS = (slice(768, 1024), slice(1024, 1152))
 BANK = 512
 
 TILES = TOKENS // P
 PAIR = 2
 PAIRS = BATCH * TILES // PAIR
 GROUP = 4
-VECTOR_ADDS_EVERY = 8
 
 FLOPS = 2 * BATCH * TOKENS * DIM * COLS
 
@@ -46,9 +48,10 @@ def tile_attention_pa_t_kernel(tc, x, f1, f2, f3, Wqkv, out_0, out_1, out_2):
 
     with ExitStack() as ctx:
         const = ctx.enter_context(tc.tile_pool(name="const", bufs=1))
-        x_pool = ctx.enter_context(tc.tile_pool(name="x", bufs=PAIRS))
+        x_pool = ctx.enter_context(tc.tile_pool(name="x", bufs=12))
         work = ctx.enter_context(tc.tile_pool(name="work", bufs=3))
-        psum = ctx.enter_context(tc.psum_pool(name="psum", bufs=2))
+        psum2 = ctx.enter_context(tc.psum_pool(name="psum2", bufs=2))
+        psum1 = ctx.enter_context(tc.psum_pool(name="psum1", bufs=1))
         ctx.enter_context(tc.manual_schedule())
 
         def load_x_pair(i):
@@ -59,7 +62,8 @@ def tile_attention_pa_t_kernel(tc, x, f1, f2, f3, Wqkv, out_0, out_1, out_2):
             return x_pair
 
         w_rows = const.tile([P, PASSES * PACK, COLS], BF16)
-        for g in range(PASSES):
+
+        def load_w(g):
             by_partition = Wqkv[K_PASS * g : K_PASS * (g + 1), :].rearrange(
                 "(p t) c -> p t c", t=PACK
             )
@@ -69,27 +73,15 @@ def tile_attention_pa_t_kernel(tc, x, f1, f2, f3, Wqkv, out_0, out_1, out_2):
                     in_=by_partition[:, 2 * u : 2 * u + 2, :],
                 )
 
+        angle0 = const.tile([P, TILES, AXIS_DIM], BF16)
+        late_angles = const.tile([P, 2, TILES, AXIS_DIM], BF16)
+        by_token = "(p t) j -> p t j"
+        nc.sync.dma_start(out=angle0[:], in_=f1.rearrange(by_token, t=TILES))
+        load_w(0)
         x_pairs = [load_x_pair(0)]
-
-        angles = const.tile([P, AXES, TILES, AXIS_DIM], BF16)
-        for axis, f in enumerate((f1, f2, f3)):
-            nc.sync.dma_start(out=angles[:, axis], in_=f.rearrange("(p t) j -> p t j", t=TILES))
-
-        for i in range(1, PAIRS):
-            x_pairs.append(load_x_pair(i))
-
-        factors = const.tile([P, TILES, 2, HEAD_DIM], F32)
-
-        def make_factors(group):
-            tiles = slice(GROUP * group, GROUP * (group + 1))
-            angle = angles[:, :, tiles, :].rearrange("p a t j -> p t a j")
-            own = factors[:, tiles, 0, :].rearrange("p t (a j) -> p t a j", a=AXES)
-            partner = factors[:, tiles, 1, :].rearrange("p t (a j) -> p t a j", a=AXES)
-            nc.scalar.activation(out=own, in_=angle, func=SIN, bias=math.pi / 2, scale=-1.0)
-            nc.scalar.activation(out=partner[:, :, :, :HALF], in_=angle[:, :, :, HALF:], func=SIN)
-            nc.scalar.activation(
-                out=partner[:, :, :, HALF:], in_=angle[:, :, :, :HALF], func=SIN, scale=-1.0
-            )
+        load_w(1)
+        nc.sync.dma_start(out=late_angles[:, 0], in_=f2.rearrange(by_token, t=TILES))
+        nc.sync.dma_start(out=late_angles[:, 1], in_=f3.rearrange(by_token, t=TILES))
 
         warm = const.tile([P, 1], F32)
         nc.vector.memset(warm[:], 0.0)
@@ -97,12 +89,63 @@ def tile_attention_pa_t_kernel(tc, x, f1, f2, f3, Wqkv, out_0, out_1, out_2):
 
         ident = const.tile([P, P], F32)
         make_identity(nc, ident[:])
+        ident_bf = const.tile([P, P], BF16)
+        nc.vector.tensor_copy(out=ident_bf[:], in_=ident[:])
+        partner = const.tile([P, P], F32)
+        halves = "p (h f j) -> p h f j"
+        for f in range(2):
+            nc.vector.tensor_copy(
+                out=partner[:].rearrange(halves, f=2, j=HALF)[:, :, f, :],
+                in_=ident[:].rearrange(halves, f=2, j=HALF)[:, :, 1 - f, :],
+            )
+
+        late = const.tile([P, TILES, 2, LATE_DIM], F32)
+
+        def make_late(group):
+            tiles = slice(GROUP * group, GROUP * (group + 1))
+            angle = late_angles[:, :, tiles, :].rearrange("p a t j -> p t a j")
+            own = late[:, tiles, 0, :].rearrange("p t (a j) -> p t a j", a=2)
+            other = late[:, tiles, 1, :].rearrange("p t (a j) -> p t a j", a=2)
+            nc.scalar.activation(out=own, in_=angle, func=SIN, bias=math.pi / 2, scale=-1.0)
+            nc.scalar.activation(out=other[:, :, :, :HALF], in_=angle[:, :, :, HALF:], func=SIN)
+            nc.scalar.activation(
+                out=other[:, :, :, HALF:], in_=angle[:, :, :, :HALF], func=SIN, scale=-1.0
+            )
+
+        early = const.tile([P, 2, TILES, P], F32)
+
+        def spread_angles(group):
+            tiles = slice(GROUP * group, GROUP * (group + 1))
+            spread = work.tile([P, 2, GROUP, HEADS, AXIS_DIM], BF16)
+            angle = angle0[:, tiles, :].unsqueeze(2).to_broadcast([P, GROUP, HEADS, AXIS_DIM])
+            nc.scalar.copy(out=spread[:, 0], in_=angle)
+            nc.scalar.copy(out=spread[:, 1, :, :, :HALF], in_=angle[:, :, :, HALF:])
+            nc.scalar.mul(spread[:, 1, :, :, HALF:], angle[:, :, :, :HALF], -1.0)
+            return spread
+
+        def transpose_angles(spread):
+            xt = psum2.tile([P, 2, GROUP, P], BF16)
+            for c in range(2):
+                for t in range(GROUP):
+                    nc.tensor.transpose(
+                        xt[:, c, t, :],
+                        spread[:, c, t].rearrange("p h j -> p (h j)"),
+                        ident_bf[:],
+                    )
+            return xt
+
+        def make_early(group, turned):
+            tiles = slice(GROUP * group, GROUP * (group + 1))
+            nc.scalar.activation(
+                out=early[:, 0, tiles, :], in_=turned[:, 0], func=SIN, bias=math.pi / 2, scale=-1.0
+            )
+            nc.scalar.activation(out=early[:, 1, tiles, :], in_=turned[:, 1], func=SIN)
 
         def transpose_pair(i):
-            grouped = work.tile([P, PAIR, PASSES, P, PACK], BF16, align_bytes=64)
+            grouped = work.tile([P, PASSES, PAIR, P, PACK], BF16, align_bytes=64)
             for a in range(PAIR):
                 words = x_pairs[i][:, a, :].bitcast(F32)
-                xt = psum.tile([P, PASSES * 2, P], F32)
+                xt = psum2.tile([P, PASSES * 2, P], F32)
                 for g in range(PASSES):
                     for u in range(2):
                         first = 2 * P * g + u
@@ -110,104 +153,173 @@ def tile_attention_pa_t_kernel(tc, x, f1, f2, f3, Wqkv, out_0, out_1, out_2):
                             xt[:, 2 * g + u, :], words[:, first : first + 2 * P - 1 : 2], ident[:]
                         )
                 nc.scalar.copy(
-                    out=grouped[:, a].bitcast(F32),
+                    out=grouped[:, :, a].bitcast(F32),
                     in_=xt[:].rearrange("p (g u) r -> p g r u", u=2),
                 )
             return grouped
 
         def quantise_pair(grouped):
-            x_codes = work.tile([P, PAIR, PASSES, P], U32, align_bytes=64)
-            x_scales = work.tile([P, PAIR, PASSES, P], U8, align_bytes=64)
+            x_codes = work.tile([P, PASSES, PAIR, P], U32, align_bytes=64)
+            x_scales = work.tile([P, PASSES, PAIR, P], U8, align_bytes=64)
             nc.vector.quantize_mx(
-                out=x_codes[:].rearrange("p a g r -> p (a g r)").bitcast(FP8X4),
-                scales=x_scales[:].rearrange("p a g r -> p (a g r)"),
-                in_=grouped[:].rearrange("p a g r t -> p (a g r t)"),
+                out=x_codes[:].rearrange("p g a r -> p (g a r)").bitcast(FP8X4),
+                scales=x_scales[:].rearrange("p g a r -> p (g a r)"),
+                in_=grouped[:].rearrange("p g a r t -> p (g a r t)"),
             )
             return x_codes, x_scales
-
 
         w_grouped = const.tile([P, PASSES, COLS, PACK], BF16, align_bytes=64)
         w_codes = const.tile([P, PASSES, COLS], U32, align_bytes=64)
         w_scales = const.tile([P, PASSES, COLS], U8, align_bytes=64)
 
-        def regroup_views(g, s, part):
-            c0, width = part
-            cols = slice(BLOCK * s + c0, BLOCK * s + c0 + width)
-            rows = w_rows[:, PACK * g : PACK * (g + 1), cols]
-            return (
-                w_grouped[:, g, cols, :].rearrange("p (c i) t -> p c t i", i=4),
-                rows.rearrange("p t (c i) -> p c t i", i=4),
+        def regroup_qk(g, cols, d0, width):
+            rows = w_rows[:, PACK * g : PACK * (g + 1), : 2 * BLOCK].rearrange(
+                "p t (n d) -> p n t d", d=HEAD_DIM
+            )
+            nc.vector.tensor_copy(
+                out=w_grouped[:, g, cols, :].rearrange(
+                    "p (n c i) t -> p n c t i", n=QK_HEADS, i=4
+                ),
+                in_=rows[:, :, :, d0 : d0 + width].rearrange("p n t (c i) -> p n c t i", i=4),
             )
 
-        def regroup_w(g, s):
-            wide_out, wide_in = regroup_views(g, s, PARTS[0])
-            nc.vector.tensor_copy(out=wide_out, in_=wide_in)
-            narrow_out, narrow_in = regroup_views(g, s, PARTS[1])
-            nc.scalar.copy(out=narrow_out, in_=narrow_in)
+        def regroup_v(g):
+            rows = w_rows[:, PACK * g : PACK * (g + 1), 2 * BLOCK :]
+            nc.scalar.copy(
+                out=w_grouped[:, g, 2 * BLOCK :, :].rearrange("p (c i) t -> p c t i", i=4),
+                in_=rows.rearrange("p t (c i) -> p c t i", i=4),
+            )
 
-        def quantise_w(g, s):
-            for c0, width in PARTS:
-                cols = slice(BLOCK * s + c0, BLOCK * s + c0 + width)
-                nc.vector.quantize_mx(
-                    out=w_codes[:, g, cols].bitcast(FP8X4),
-                    scales=w_scales[:, g, cols],
-                    in_=w_grouped[:, g, cols, :].rearrange("p c t -> p (c t)"),
+        def quantise_w(g, cols):
+            nc.vector.quantize_mx(
+                out=w_codes[:, g, cols].bitcast(FP8X4),
+                scales=w_scales[:, g, cols],
+                in_=w_grouped[:, g, cols, :].rearrange("p c t -> p (c t)"),
+            )
+
+        for i in range(1, PAIRS):
+            x_pairs.append(load_x_pair(i))
+
+        spread = spread_angles(0)
+        turned = transpose_angles(spread)
+        make_early(0, turned)
+        regroup_v(0)
+        regroup_qk(0, AXIS0, 0, AXIS_DIM)
+        regroup_qk(0, LATE, AXIS_DIM, LATE_DIM)
+        quantise_w(0, AXIS0)
+        quantise_w(0, LATE)
+        first_grouped = transpose_pair(0)
+        regroup_v(1)
+        regroup_qk(1, AXIS0, 0, AXIS_DIM)
+        regroup_qk(1, LATE, AXIS_DIM, LATE_DIM)
+        quantise_w(1, AXIS0)
+        ready = quantise_pair(first_grouped)
+        quantise_w(1, LATE)
+        make_late(0)
+        for g in range(PASSES):
+            for cols in V_PARTS:
+                quantise_w(g, cols)
+
+        def multiply(out, lhsT, lhsT_scale, rhs, rhs_scale):
+            for g in range(PASSES):
+                nc.tensor.matmul_mx(
+                    out=out,
+                    lhsT=lhsT(g).bitcast(FP8X4),
+                    lhsT_scale=lhsT_scale(g),
+                    rhs=rhs(g).bitcast(FP8X4),
+                    rhs_scale=rhs_scale(g),
+                    start=(g == 0),
+                    stop=(g == PASSES - 1),
                 )
 
-        pieces = [(g, s) for g in range(PASSES) for s in range(3)]
-        for n, (g, s) in enumerate(pieces):
-            regroup_w(g, s)
-            if n > 0:
-                quantise_w(*pieces[n - 1])
-        quantise_w(*pieces[-1])
-        ready = quantise_pair(transpose_pair(0))
-        make_factors(0)
+        def project_axis0(x_codes, x_scales):
+            ps_turned = psum1.tile([P, 2, PAIR * P], F32)
+            for s in range(2):
+                cols = slice(P * s, P * (s + 1))
+                multiply(
+                    ps_turned[:, s, :],
+                    lambda g: w_codes[:, g, cols],
+                    lambda g: w_scales[:, g, cols],
+                    lambda g: x_codes[:, g].rearrange("p a r -> p (a r)"),
+                    lambda g: x_scales[:, g].rearrange("p a r -> p (a r)"),
+                )
+            return ps_turned
 
-        def project(x_codes, x_scales, a):
-            ps_q = psum.tile([P, BANK], F32)
-            ps_k = psum.tile([P, BANK], F32)
-            ps_v = psum.tile([P, BANK], F32)
-            for s, bank in enumerate((ps_q, ps_k, ps_v)):
-                for c0, width in PARTS:
-                    cols = slice(BLOCK * s + c0, BLOCK * s + c0 + width)
-                    for g in range(PASSES):
-                        nc.tensor.matmul_mx(
-                            out=bank[:, c0 : c0 + width],
-                            lhsT=x_codes[:, a, g, :].bitcast(FP8X4),
-                            lhsT_scale=x_scales[:, a, g, :],
-                            rhs=w_codes[:, g, cols].bitcast(FP8X4),
-                            rhs_scale=w_scales[:, g, cols],
-                            start=(g == 0),
-                            stop=(g == PASSES - 1),
+        def project_tile(x_codes, x_scales, a):
+            ps_late = psum2.tile([P, BANK], F32)
+            ps_v = psum2.tile([P, BANK], F32)
+            for bank, parts in ((ps_late, (LATE,)), (ps_v, V_PARTS)):
+                c0 = parts[0].start
+                for cols in parts:
+                    multiply(
+                        bank[:, cols.start - c0 : cols.stop - c0],
+                        lambda g: x_codes[:, g, a, :],
+                        lambda g: x_scales[:, g, a, :],
+                        lambda g: w_codes[:, g, cols],
+                        lambda g: w_scales[:, g, cols],
+                    )
+            return ps_late, ps_v
+
+        def products_axis0(ps_turned, t0):
+            early_products = work.tile([P, 2, 2, PAIR * P], F32)
+            shape = [P, 2, 2, PAIR * P]
+            pair_factors = early[:, :, t0 : t0 + PAIR, :].rearrange("p c t r -> p c (t r)")
+            nc.vector.tensor_tensor(
+                out=early_products[:],
+                in0=ps_turned[:].unsqueeze(1).to_broadcast(shape),
+                in1=pair_factors.unsqueeze(2).to_broadcast(shape),
+                op=MULT,
+            )
+            return early_products
+
+        def add_axis0(early_products, staged, slot0):
+            ps_back = psum1.tile([P, PAIR, 2, P], F32)
+            for a in range(PAIR):
+                for s in range(2):
+                    for c, order in enumerate((ident, partner)):
+                        nc.tensor.matmul(
+                            ps_back[:, a, s, :],
+                            lhsT=early_products[:, c, s, P * a : P * (a + 1)],
+                            rhs=order[:],
+                            start=(c == 0),
+                            stop=(c == 1),
+                            is_transpose=True,
                         )
-            return ps_q, ps_k, ps_v
-
-        def rope_and_collect(banks, t, staged, slot):
-            ps_q, ps_k, ps_v = banks
-            products = work.tile([P, 2, 2, BLOCK], F32)
-            shape = [P, 2, HEADS, HEAD_DIM]
-            for s, bank in enumerate((ps_q, ps_k)):
-                by_head = bank[:, :BLOCK].rearrange("p (h d) -> p h d", h=HEADS)
-                nc.vector.tensor_tensor(
-                    out=products[:, :, s, :].rearrange("p c (h d) -> p c h d", h=HEADS),
-                    in0=by_head.unsqueeze(1).to_broadcast(shape),
-                    in1=factors[:, t].unsqueeze(2).to_broadcast(shape),
-                    op=MULT,
-                )
-            split = "p s (h a f j) -> p (s h) a f j"
-            own_part = products[:, 0].rearrange(split, h=HEADS, a=AXES, f=2)
-            partner_part = products[:, 1].rearrange(split, h=HEADS, a=AXES, f=2)
-            rotated = staged[:, 0:2, :, slot, :].rearrange(
-                "p s h (a f j) -> p (s h) a f j", a=AXES, f=2
+            nc.scalar.copy(
+                out=staged[:, 0:2, :, slot0 : slot0 + PAIR, :AXIS_DIM].rearrange(
+                    "p s h t j -> p t (s h) j"
+                ),
+                in_=ps_back[:].rearrange("p t s (h j) -> p t (s h) j", h=HEADS),
             )
-            adder = nc.vector if t % VECTOR_ADDS_EVERY == VECTOR_ADDS_EVERY - 1 else nc.gpsimd
+
+        def products_late(ps_late, t):
+            products = work.tile([P, 2, QK_HEADS, LATE_DIM], F32)
+            shape = [P, 2, QK_HEADS, LATE_DIM]
+            by_head = ps_late[:].rearrange("p (n d) -> p n d", n=QK_HEADS)
+            nc.vector.tensor_tensor(
+                out=products[:],
+                in0=by_head.unsqueeze(1).to_broadcast(shape),
+                in1=late[:, t].unsqueeze(2).to_broadcast(shape),
+                op=MULT,
+            )
+            return products
+
+        def add_late(products, staged, slot):
+            split = "p n (a f j) -> p n a f j"
+            own_part = products[:, 0].rearrange(split, a=2, f=2)
+            partner_part = products[:, 1].rearrange(split, a=2, f=2)
+            rotated = staged[:, 0:2, :, slot, AXIS_DIM:].rearrange(
+                "p s h (a f j) -> p (s h) a f j", a=2, f=2
+            )
             for f in range(2):
-                adder.tensor_tensor(
+                nc.gpsimd.tensor_tensor(
                     out=rotated[:, :, :, f, :],
                     in0=own_part[:, :, :, f, :],
                     in1=partner_part[:, :, :, 1 - f, :],
                     op=ADD,
                 )
+
+        def collect_v(ps_v, staged, slot):
             nc.scalar.copy(
                 out=staged[:, 2, :, slot, :],
                 in_=ps_v[:, :BLOCK].rearrange("p (h d) -> p h d", h=HEADS),
@@ -226,16 +338,26 @@ def tile_attention_pa_t_kernel(tc, x, f1, f2, f3, Wqkv, out_0, out_1, out_2):
             x_codes, x_scales = ready
             b, t0 = divmod(i * PAIR, TILES)
             slot0 = t0 % GROUP
+            next_group = t0 // GROUP + 1
+            makes_factors = b == 0 and next_group < TILES // GROUP
             if slot0 == 0:
                 staged = work.tile([P, 3, HEADS, GROUP, HEAD_DIM], F32)
-                next_group = t0 // GROUP + 1
-                if b == 0 and next_group < TILES // GROUP:
-                    make_factors(next_group)
             grouped = transpose_pair(i + 1) if i + 1 < PAIRS else None
-            rope_and_collect(project(x_codes, x_scales, 0), t0, staged, slot0)
+            early_products = products_axis0(project_axis0(x_codes, x_scales), t0)
+            ps_late, ps_v = project_tile(x_codes, x_scales, 0)
+            add_late(products_late(ps_late, t0), staged, slot0)
+            collect_v(ps_v, staged, slot0)
+            if makes_factors and slot0 == 0:
+                make_late(next_group)
+                spread = spread_angles(next_group)
+            elif makes_factors:
+                make_early(next_group, transpose_angles(spread))
             if grouped is not None:
                 ready = quantise_pair(grouped)
-            rope_and_collect(project(x_codes, x_scales, 1), t0 + 1, staged, slot0 + 1)
+            ps_late, ps_v = project_tile(x_codes, x_scales, 1)
+            add_late(products_late(ps_late, t0 + 1), staged, slot0 + 1)
+            collect_v(ps_v, staged, slot0 + 1)
+            add_axis0(early_products, staged, slot0)
             if i * PAIR >= BATCH * TILES - GROUP:
                 store(b, t0, PAIR, staged, slot0)
             elif slot0 + PAIR == GROUP:

@@ -311,13 +311,9 @@ def tile_attention_pa_t_kernel(tc, x, f1, f2, f3, Wqkv, out_0, out_1, out_2):
             rotated = staged[:, 0:2, :, slot, AXIS_DIM:].rearrange(
                 "p s h (a f j) -> p (s h) a f j", a=2, f=2
             )
-            for f in range(2):
-                nc.gpsimd.tensor_tensor(
-                    out=rotated[:, :, :, f, :],
-                    in0=own_part[:, :, :, f, :],
-                    in1=partner_part[:, :, :, 1 - f, :],
-                    op=ADD,
-                )
+            nc.gpsimd.tensor_tensor(
+                out=rotated, in0=own_part, in1=partner_part[:, :, :, ::-1, :], op=ADD
+            )
 
         def collect_v(ps_v, staged, slot):
             nc.scalar.copy(

@@ -18,7 +18,8 @@ TOKENS = 2048
 DIM = 1024
 HEADS = 4
 HEAD_DIM = 96
-AXIS_DIM = 32
+AXES = 3
+AXIS_DIM = HEAD_DIM // AXES
 HALF = AXIS_DIM // 2
 LATE_DIM = HEAD_DIM - AXIS_DIM
 QK_HEADS = 2 * HEADS
@@ -38,6 +39,7 @@ TILES = TOKENS // P
 PAIR = 2
 PAIRS = BATCH * TILES // PAIR
 GROUP = 4
+GROUPS = TILES // GROUP
 
 FLOPS = 2 * BATCH * TOKENS * DIM * COLS
 
@@ -50,8 +52,7 @@ def tile_attention_pa_t_kernel(tc, x, f1, f2, f3, Wqkv, out_0, out_1, out_2):
         const = ctx.enter_context(tc.tile_pool(name="const", bufs=1))
         x_pool = ctx.enter_context(tc.tile_pool(name="x", bufs=12))
         work = ctx.enter_context(tc.tile_pool(name="work", bufs=3))
-        psum2 = ctx.enter_context(tc.psum_pool(name="psum2", bufs=2))
-        psum1 = ctx.enter_context(tc.psum_pool(name="psum1", bufs=1))
+        psum = ctx.enter_context(tc.psum_pool(name="psum", bufs=2))
         ctx.enter_context(tc.manual_schedule())
 
         def load_x_pair(i):
@@ -61,27 +62,22 @@ def tile_attention_pa_t_kernel(tc, x, f1, f2, f3, Wqkv, out_0, out_1, out_2):
             nc.sync.dma_start(out=x_pair[:], in_=by_partition[:, t : t + PAIR, :])
             return x_pair
 
-        w_rows = const.tile([P, PASSES * PACK, COLS], BF16)
-
-        def load_w(g):
+        def load_w(g, cols):
+            w_rows = const.tile([P, PACK, cols.stop - cols.start], BF16, name="w%d_%d" % (g, cols.start))
             by_partition = Wqkv[K_PASS * g : K_PASS * (g + 1), :].rearrange(
                 "(p t) c -> p t c", t=PACK
             )
-            for u in range(2):
-                nc.sync.dma_start(
-                    out=w_rows[:, PACK * g + 2 * u : PACK * g + 2 * u + 2, :],
-                    in_=by_partition[:, 2 * u : 2 * u + 2, :],
-                )
+            nc.sync.dma_start(out=w_rows[:], in_=by_partition[:, :, cols])
+            return w_rows
 
-        angle0 = const.tile([P, TILES, AXIS_DIM], BF16)
-        late_angles = const.tile([P, 2, TILES, AXIS_DIM], BF16)
-        by_token = "(p t) j -> p t j"
-        nc.sync.dma_start(out=angle0[:], in_=f1.rearrange(by_token, t=TILES))
-        load_w(0)
+        qk_rows = [load_w(g, slice(0, 2 * BLOCK)) for g in range(PASSES)]
         x_pairs = [load_x_pair(0)]
-        load_w(1)
-        nc.sync.dma_start(out=late_angles[:, 0], in_=f2.rearrange(by_token, t=TILES))
-        nc.sync.dma_start(out=late_angles[:, 1], in_=f3.rearrange(by_token, t=TILES))
+        angles = const.tile([P, AXES, TILES, AXIS_DIM], BF16)
+        for axis, f in enumerate((f1, f2, f3)):
+            nc.sync.dma_start(out=angles[:, axis], in_=f.rearrange("(p t) j -> p t j", t=TILES))
+        v_rows = [load_w(g, slice(2 * BLOCK, COLS)) for g in range(PASSES)]
+        for i in range(1, PAIRS):
+            x_pairs.append(load_x_pair(i))
 
         warm = const.tile([P, 1], F32)
         nc.vector.memset(warm[:], 0.0)
@@ -99,59 +95,71 @@ def tile_attention_pa_t_kernel(tc, x, f1, f2, f3, Wqkv, out_0, out_1, out_2):
                 in_=ident[:].rearrange(halves, f=2, j=HALF)[:, :, 1 - f, :],
             )
 
-        late = const.tile([P, TILES, 2, LATE_DIM], F32)
-
-        def make_late(group):
-            tiles = slice(GROUP * group, GROUP * (group + 1))
-            angle = late_angles[:, :, tiles, :].rearrange("p a t j -> p t a j")
-            own = late[:, tiles, 0, :].rearrange("p t (a j) -> p t a j", a=2)
-            other = late[:, tiles, 1, :].rearrange("p t (a j) -> p t a j", a=2)
+        def make_factors(own, other, angle):
             nc.scalar.activation(out=own, in_=angle, func=SIN, bias=math.pi / 2, scale=-1.0)
             nc.scalar.activation(out=other[:, :, :, :HALF], in_=angle[:, :, :, HALF:], func=SIN)
             nc.scalar.activation(
                 out=other[:, :, :, HALF:], in_=angle[:, :, :, :HALF], func=SIN, scale=-1.0
             )
 
-        early = const.tile([P, 2, TILES, P], F32)
+        late = const.tile([P, TILES, 2, LATE_DIM], F32)
+        even = const.tile([P, GROUPS, 2, PAIR, AXIS_DIM], F32)
+        odd = const.tile([P, 2, GROUPS, PAIR, P], F32)
+
+        def make_token_factors(group):
+            tiles = slice(GROUP * group, GROUP * (group + 1))
+            by_axis = "p t (a j) -> p t a j"
+            make_factors(
+                late[:, tiles, 0, :].rearrange(by_axis, a=AXES - 1),
+                late[:, tiles, 1, :].rearrange(by_axis, a=AXES - 1),
+                angles[:, 1:, tiles, :].rearrange("p a t j -> p t a j"),
+            )
+            pair = slice(GROUP * group, GROUP * group + PAIR)
+            make_factors(
+                even[:, group, 0].unsqueeze(1),
+                even[:, group, 1].unsqueeze(1),
+                angles[:, 0, pair, :].unsqueeze(1),
+            )
 
         def spread_angles(group):
-            tiles = slice(GROUP * group, GROUP * (group + 1))
-            spread = work.tile([P, 2, GROUP, HEADS, AXIS_DIM], BF16)
-            angle = angle0[:, tiles, :].unsqueeze(2).to_broadcast([P, GROUP, HEADS, AXIS_DIM])
+            spread = work.tile([P, 2, PAIR, HEADS, AXIS_DIM], BF16)
+            tiles = slice(GROUP * group + PAIR, GROUP * (group + 1))
+            angle = angles[:, 0, tiles, :].unsqueeze(2).to_broadcast([P, PAIR, HEADS, AXIS_DIM])
             nc.scalar.copy(out=spread[:, 0], in_=angle)
             nc.scalar.copy(out=spread[:, 1, :, :, :HALF], in_=angle[:, :, :, HALF:])
             nc.scalar.mul(spread[:, 1, :, :, HALF:], angle[:, :, :, :HALF], -1.0)
             return spread
 
-        def transpose_angles(spread):
-            xt = psum2.tile([P, 2, GROUP, P], BF16)
+        def make_channel_factors(group, spread):
+            xt = psum.tile([P, 2, PAIR, P], BF16)
             for c in range(2):
-                for t in range(GROUP):
+                for a in range(PAIR):
                     nc.tensor.transpose(
-                        xt[:, c, t, :],
-                        spread[:, c, t].rearrange("p h j -> p (h j)"),
-                        ident_bf[:],
+                        xt[:, c, a, :], spread[:, c, a].rearrange("p h j -> p (h j)"), ident_bf[:]
                     )
-            return xt
-
-        def make_early(group, turned):
-            tiles = slice(GROUP * group, GROUP * (group + 1))
             nc.scalar.activation(
-                out=early[:, 0, tiles, :], in_=turned[:, 0], func=SIN, bias=math.pi / 2, scale=-1.0
+                out=odd[:, 0, group], in_=xt[:, 0], func=SIN, bias=math.pi / 2, scale=-1.0
             )
-            nc.scalar.activation(out=early[:, 1, tiles, :], in_=turned[:, 1], func=SIN)
+            nc.scalar.activation(out=odd[:, 1, group], in_=xt[:, 1], func=SIN)
+
+        sorted_words = {}
+
+        def words_in_place(i):
+            return x_pairs[i][:].bitcast(F32).rearrange("p a (g w u) -> p a g u w", g=PASSES, u=2)
+
+        def sort_words(i):
+            words = work.tile([P, PAIR, PASSES, 2, P], F32)
+            nc.scalar.copy(out=words[:], in_=words_in_place(i))
+            sorted_words[i] = words
 
         def transpose_pair(i):
+            words = sorted_words[i] if i in sorted_words else words_in_place(i)
             grouped = work.tile([P, PASSES, PAIR, P, PACK], BF16, align_bytes=64)
             for a in range(PAIR):
-                words = x_pairs[i][:, a, :].bitcast(F32)
-                xt = psum2.tile([P, PASSES * 2, P], F32)
+                xt = psum.tile([P, PASSES * 2, P], F32)
                 for g in range(PASSES):
                     for u in range(2):
-                        first = 2 * P * g + u
-                        nc.tensor.transpose(
-                            xt[:, 2 * g + u, :], words[:, first : first + 2 * P - 1 : 2], ident[:]
-                        )
+                        nc.tensor.transpose(xt[:, 2 * g + u, :], words[:, a, g, u, :], ident[:])
                 nc.scalar.copy(
                     out=grouped[:, :, a].bitcast(F32),
                     in_=xt[:].rearrange("p (g u) r -> p g r u", u=2),
@@ -172,11 +180,9 @@ def tile_attention_pa_t_kernel(tc, x, f1, f2, f3, Wqkv, out_0, out_1, out_2):
         w_codes = const.tile([P, PASSES, COLS], U32, align_bytes=64)
         w_scales = const.tile([P, PASSES, COLS], U8, align_bytes=64)
 
-        def regroup_qk(g, cols, d0, width):
-            rows = w_rows[:, PACK * g : PACK * (g + 1), : 2 * BLOCK].rearrange(
-                "p t (n d) -> p n t d", d=HEAD_DIM
-            )
-            nc.vector.tensor_copy(
+        def regroup_qk(copy, g, cols, d0, width):
+            rows = qk_rows[g][:].rearrange("p t (n d) -> p n t d", d=HEAD_DIM)
+            copy(
                 out=w_grouped[:, g, cols, :].rearrange(
                     "p (n c i) t -> p n c t i", n=QK_HEADS, i=4
                 ),
@@ -184,10 +190,9 @@ def tile_attention_pa_t_kernel(tc, x, f1, f2, f3, Wqkv, out_0, out_1, out_2):
             )
 
         def regroup_v(g):
-            rows = w_rows[:, PACK * g : PACK * (g + 1), 2 * BLOCK :]
             nc.scalar.copy(
                 out=w_grouped[:, g, 2 * BLOCK :, :].rearrange("p (c i) t -> p c t i", i=4),
-                in_=rows.rearrange("p t (c i) -> p c t i", i=4),
+                in_=v_rows[g][:].rearrange("p t (c i) -> p c t i", i=4),
             )
 
         def quantise_w(g, cols):
@@ -196,29 +201,6 @@ def tile_attention_pa_t_kernel(tc, x, f1, f2, f3, Wqkv, out_0, out_1, out_2):
                 scales=w_scales[:, g, cols],
                 in_=w_grouped[:, g, cols, :].rearrange("p c t -> p (c t)"),
             )
-
-        for i in range(1, PAIRS):
-            x_pairs.append(load_x_pair(i))
-
-        spread = spread_angles(0)
-        turned = transpose_angles(spread)
-        make_early(0, turned)
-        regroup_v(0)
-        regroup_qk(0, AXIS0, 0, AXIS_DIM)
-        regroup_qk(0, LATE, AXIS_DIM, LATE_DIM)
-        quantise_w(0, AXIS0)
-        quantise_w(0, LATE)
-        first_grouped = transpose_pair(0)
-        regroup_v(1)
-        regroup_qk(1, AXIS0, 0, AXIS_DIM)
-        regroup_qk(1, LATE, AXIS_DIM, LATE_DIM)
-        quantise_w(1, AXIS0)
-        ready = quantise_pair(first_grouped)
-        quantise_w(1, LATE)
-        make_late(0)
-        for g in range(PASSES):
-            for cols in V_PARTS:
-                quantise_w(g, cols)
 
         def multiply(out, lhsT, lhsT_scale, rhs, rhs_scale):
             for g in range(PASSES):
@@ -232,67 +214,87 @@ def tile_attention_pa_t_kernel(tc, x, f1, f2, f3, Wqkv, out_0, out_1, out_2):
                     stop=(g == PASSES - 1),
                 )
 
-        def project_axis0(x_codes, x_scales):
-            ps_turned = psum1.tile([P, 2, PAIR * P], F32)
-            for s in range(2):
-                cols = slice(P * s, P * (s + 1))
-                multiply(
-                    ps_turned[:, s, :],
-                    lambda g: w_codes[:, g, cols],
-                    lambda g: w_scales[:, g, cols],
-                    lambda g: x_codes[:, g].rearrange("p a r -> p (a r)"),
-                    lambda g: x_scales[:, g].rearrange("p a r -> p (a r)"),
-                )
-            return ps_turned
+        def project(out, quantised, a, cols):
+            x_codes, x_scales = quantised
+            multiply(
+                out,
+                lambda g: x_codes[:, g, a, :],
+                lambda g: x_scales[:, g, a, :],
+                lambda g: w_codes[:, g, cols],
+                lambda g: w_scales[:, g, cols],
+            )
 
-        def project_tile(x_codes, x_scales, a):
-            ps_late = psum2.tile([P, BANK], F32)
-            ps_v = psum2.tile([P, BANK], F32)
-            for bank, parts in ((ps_late, (LATE,)), (ps_v, V_PARTS)):
-                c0 = parts[0].start
-                for cols in parts:
-                    multiply(
-                        bank[:, cols.start - c0 : cols.stop - c0],
-                        lambda g: x_codes[:, g, a, :],
-                        lambda g: x_scales[:, g, a, :],
-                        lambda g: w_codes[:, g, cols],
-                        lambda g: w_scales[:, g, cols],
-                    )
-            return ps_late, ps_v
+        def project_turned(out, quantised, cols):
+            x_codes, x_scales = quantised
+            multiply(
+                out,
+                lambda g: w_codes[:, g, cols],
+                lambda g: w_scales[:, g, cols],
+                lambda g: x_codes[:, g].rearrange("p a r -> p (a r)"),
+                lambda g: x_scales[:, g].rearrange("p a r -> p (a r)"),
+            )
 
-        def products_axis0(ps_turned, t0):
-            early_products = work.tile([P, 2, 2, PAIR * P], F32)
-            shape = [P, 2, 2, PAIR * P]
-            pair_factors = early[:, :, t0 : t0 + PAIR, :].rearrange("p c t r -> p c (t r)")
+        def rope_even(quantised, group, staged):
+            axis0 = psum.tile([P, PAIR, QK_HEADS, AXIS_DIM], F32)
+            for a in range(PAIR):
+                project(axis0[:, a].rearrange("p n j -> p (n j)"), quantised, a, AXIS0)
+            axis0_products = work.tile([P, 2, PAIR, QK_HEADS, AXIS_DIM], F32)
+            shape = [P, 2, PAIR, QK_HEADS, AXIS_DIM]
             nc.vector.tensor_tensor(
-                out=early_products[:],
-                in0=ps_turned[:].unsqueeze(1).to_broadcast(shape),
-                in1=pair_factors.unsqueeze(2).to_broadcast(shape),
+                out=axis0_products[:],
+                in0=axis0[:].unsqueeze(1).to_broadcast(shape),
+                in1=even[:, group].unsqueeze(3).to_broadcast(shape),
                 op=MULT,
             )
-            return early_products
+            halved = "p t n (f j) -> p t n f j"
+            nc.gpsimd.tensor_tensor(
+                out=staged[:, 0:2, :, :PAIR, :AXIS_DIM].rearrange(
+                    "p s h t (f j) -> p t (s h) f j", f=2
+                ),
+                in0=axis0_products[:, 0].rearrange(halved, f=2),
+                in1=axis0_products[:, 1].rearrange(halved, f=2)[:, :, :, ::-1, :],
+                op=ADD,
+            )
 
-        def add_axis0(early_products, staged, slot0):
-            ps_back = psum1.tile([P, PAIR, 2, P], F32)
+        def products_odd(quantised, group):
+            axis0 = psum.tile([P, 2, PAIR * P], F32)
+            for s in range(2):
+                project_turned(axis0[:, s, :], quantised, slice(P * s, P * (s + 1)))
+            axis0_products = work.tile([P, 2, 2, PAIR * P], F32)
+            shape = [P, 2, 2, PAIR * P]
+            factors = odd[:, :, group].rearrange("p c t r -> p c (t r)")
+            nc.vector.tensor_tensor(
+                out=axis0_products[:],
+                in0=axis0[:].unsqueeze(1).to_broadcast(shape),
+                in1=factors.unsqueeze(2).to_broadcast(shape),
+                op=MULT,
+            )
+            return axis0_products
+
+        def add_odd(axis0_products):
+            axis0 = psum.tile([P, PAIR, 2, P], F32)
             for a in range(PAIR):
                 for s in range(2):
                     for c, order in enumerate((ident, partner)):
                         nc.tensor.matmul(
-                            ps_back[:, a, s, :],
-                            lhsT=early_products[:, c, s, P * a : P * (a + 1)],
+                            axis0[:, a, s, :],
+                            lhsT=axis0_products[:, c, s, P * a : P * (a + 1)],
                             rhs=order[:],
                             start=(c == 0),
                             stop=(c == 1),
                             is_transpose=True,
                         )
+            return axis0
+
+        def collect_odd(axis0, staged):
             nc.scalar.copy(
-                out=staged[:, 0:2, :, slot0 : slot0 + PAIR, :AXIS_DIM].rearrange(
-                    "p s h t j -> p t (s h) j"
-                ),
-                in_=ps_back[:].rearrange("p t s (h j) -> p t (s h) j", h=HEADS),
+                out=staged[:, 0:2, :, PAIR:, :AXIS_DIM].rearrange("p s h t j -> p t (s h) j"),
+                in_=axis0[:].rearrange("p t s (h j) -> p t (s h) j", h=HEADS),
             )
 
-        def products_late(ps_late, t):
+        def rope_late(quantised, a, t, staged, adder):
+            ps_late = psum.tile([P, BANK], F32)
+            project(ps_late[:], quantised, a, LATE)
             products = work.tile([P, 2, QK_HEADS, LATE_DIM], F32)
             shape = [P, 2, QK_HEADS, LATE_DIM]
             by_head = ps_late[:].rearrange("p (n d) -> p n d", n=QK_HEADS)
@@ -302,59 +304,91 @@ def tile_attention_pa_t_kernel(tc, x, f1, f2, f3, Wqkv, out_0, out_1, out_2):
                 in1=late[:, t].unsqueeze(2).to_broadcast(shape),
                 op=MULT,
             )
-            return products
-
-        def add_late(products, staged, slot):
             split = "p n (a f j) -> p n a f j"
-            own_part = products[:, 0].rearrange(split, a=2, f=2)
-            partner_part = products[:, 1].rearrange(split, a=2, f=2)
-            rotated = staged[:, 0:2, :, slot, AXIS_DIM:].rearrange(
-                "p s h (a f j) -> p (s h) a f j", a=2, f=2
-            )
-            nc.gpsimd.tensor_tensor(
-                out=rotated, in0=own_part, in1=partner_part[:, :, :, ::-1, :], op=ADD
+            adder.tensor_tensor(
+                out=staged[:, 0:2, :, t % GROUP, AXIS_DIM:].rearrange(
+                    "p s h (a f j) -> p (s h) a f j", a=AXES - 1, f=2
+                ),
+                in0=products[:, 0].rearrange(split, a=AXES - 1, f=2),
+                in1=products[:, 1].rearrange(split, a=AXES - 1, f=2)[:, :, :, ::-1, :],
+                op=ADD,
             )
 
-        def collect_v(ps_v, staged, slot):
+        def collect_v(quantised, a, slot, staged):
+            ps_v = psum.tile([P, BANK], F32)
+            for cols in V_PARTS:
+                project(
+                    ps_v[:, cols.start - 2 * BLOCK : cols.stop - 2 * BLOCK], quantised, a, cols
+                )
             nc.scalar.copy(
                 out=staged[:, 2, :, slot, :],
                 in_=ps_v[:, :BLOCK].rearrange("p (h d) -> p h d", h=HEADS),
             )
 
-        def store(b, t0, count, staged, slot0):
-            for s, out in enumerate(outs):
-                by_partition = out[b].rearrange("h (p t) d -> p h t d", t=TILES)
+        def store(b, t0, count, staged):
+            slot0 = t0 % GROUP
+            for s in (2, 0, 1):
+                by_partition = outs[s][b].rearrange("h (p t) d -> p h t d", t=TILES)
                 nc.sync.dma_start(
                     out=by_partition[:, :, t0 : t0 + count, :],
                     in_=staged[:, s, :, slot0 : slot0 + count, :],
                 )
 
-        staged = None
+        for g in range(PASSES):
+            regroup_qk(nc.scalar.copy, g, AXIS0, 0, AXIS_DIM)
+            regroup_qk(nc.vector.tensor_copy, g, LATE, AXIS_DIM, LATE_DIM)
+            quantise_w(g, LATE)
+            quantise_w(g, AXIS0)
+        quantised = quantise_pair(transpose_pair(0))
+        make_token_factors(0)
+        for g in range(PASSES):
+            regroup_v(g)
+
+        before = None
+        grouped = {}
         for i in range(PAIRS):
-            x_codes, x_scales = ready
             b, t0 = divmod(i * PAIR, TILES)
-            slot0 = t0 % GROUP
-            next_group = t0 // GROUP + 1
-            makes_factors = b == 0 and next_group < TILES // GROUP
-            if slot0 == 0:
+            group, slot0 = divmod(t0, GROUP)
+            even_pair = slot0 == 0
+            if i + 3 < PAIRS and (i + 3) * PAIR >= TILES:
+                sort_words(i + 3)
+            if even_pair:
                 staged = work.tile([P, 3, HEADS, GROUP, HEAD_DIM], F32)
-            grouped = transpose_pair(i + 1) if i + 1 < PAIRS else None
-            early_products = products_axis0(project_axis0(x_codes, x_scales), t0)
-            ps_late, ps_v = project_tile(x_codes, x_scales, 0)
-            add_late(products_late(ps_late, t0), staged, slot0)
-            collect_v(ps_v, staged, slot0)
-            if makes_factors and slot0 == 0:
-                make_late(next_group)
-                spread = spread_angles(next_group)
-            elif makes_factors:
-                make_early(next_group, transpose_angles(spread))
-            if grouped is not None:
-                ready = quantise_pair(grouped)
-            ps_late, ps_v = project_tile(x_codes, x_scales, 1)
-            add_late(products_late(ps_late, t0 + 1), staged, slot0 + 1)
-            collect_v(ps_v, staged, slot0 + 1)
-            add_axis0(early_products, staged, slot0)
-            if i * PAIR >= BATCH * TILES - GROUP:
-                store(b, t0, PAIR, staged, slot0)
-            elif slot0 + PAIR == GROUP:
-                store(b, t0 + PAIR - GROUP, GROUP, staged, 0)
+                rope_even(quantised, group, staged)
+                spread = spread_angles(group) if b == 0 else None
+            else:
+                odd_products = products_odd(quantised, group)
+                if b == 0 and group + 1 < GROUPS:
+                    make_token_factors(group + 1)
+            rope_late(quantised, 0, t0, staged, nc.gpsimd)
+            if i == 0:
+                grouped[1] = transpose_pair(1)
+            else:
+                collect_v(before[0], 0, before[2], before[1])
+                coming = quantise_pair(grouped[i + 1]) if i + 1 < PAIRS else None
+            if i > 0 and i + 2 < PAIRS:
+                grouped[i + 2] = transpose_pair(i + 2)
+            rope_late(
+                quantised, 1, t0 + 1, staged, nc.gpsimd if i + 1 < PAIRS else nc.vector
+            )
+            if i == 0:
+                coming = quantise_pair(grouped[1])
+                grouped[2] = transpose_pair(2)
+                for g in range(PASSES):
+                    for cols in V_PARTS:
+                        quantise_w(g, cols)
+            else:
+                collect_v(before[0], 1, before[2] + 1, before[1])
+            if not even_pair:
+                collect_odd(add_odd(odd_products), staged)
+            if even_pair and b == 0:
+                make_channel_factors(group, spread)
+            if even_pair and i > 0:
+                last_b, last_t = divmod((i - 2) * PAIR, TILES)
+                store(last_b, last_t, GROUP, before[1])
+            before = (quantised, staged, slot0)
+            quantised = coming
+        store(BATCH - 1, TILES - GROUP, PAIR, staged)
+        for a in range(PAIR):
+            collect_v(before[0], a, PAIR + a, staged)
+        store(BATCH - 1, TILES - PAIR, PAIR, staged)

@@ -40,6 +40,7 @@ PAIR = 2
 PAIRS = BATCH * TILES // PAIR
 GROUP = 4
 GROUPS = TILES // GROUP
+SORTED_FROM = 5
 
 FLOPS = 2 * BATCH * TOKENS * DIM * COLS
 
@@ -70,13 +71,16 @@ def tile_attention_pa_t_kernel(tc, x, f1, f2, f3, Wqkv, out_0, out_1, out_2):
             nc.sync.dma_start(out=w_rows[:], in_=by_partition[:, :, cols])
             return w_rows
 
-        qk_rows = [load_w(g, slice(0, 2 * BLOCK)) for g in range(PASSES)]
         x_pairs = [load_x_pair(0)]
+        qk_rows = [load_w(g, slice(0, 2 * BLOCK)) for g in range(PASSES)]
         angles = const.tile([P, AXES, TILES, AXIS_DIM], BF16)
         for axis, f in enumerate((f1, f2, f3)):
             nc.sync.dma_start(out=angles[:, axis], in_=f.rearrange("(p t) j -> p t j", t=TILES))
-        v_rows = [load_w(g, slice(2 * BLOCK, COLS)) for g in range(PASSES)]
-        for i in range(1, PAIRS):
+        v_rows = []
+        for g in range(PASSES):
+            v_rows.append(load_w(g, slice(2 * BLOCK, COLS)))
+            x_pairs.append(load_x_pair(1 + g))
+        for i in range(1 + PASSES, PAIRS):
             x_pairs.append(load_x_pair(i))
 
         warm = const.tile([P, 1], F32)
@@ -86,14 +90,15 @@ def tile_attention_pa_t_kernel(tc, x, f1, f2, f3, Wqkv, out_0, out_1, out_2):
         ident = const.tile([P, P], F32)
         make_identity(nc, ident[:])
         ident_bf = const.tile([P, P], BF16)
-        nc.vector.tensor_copy(out=ident_bf[:], in_=ident[:])
         partner = const.tile([P, P], F32)
-        halves = "p (h f j) -> p h f j"
-        for f in range(2):
-            nc.vector.tensor_copy(
-                out=partner[:].rearrange(halves, f=2, j=HALF)[:, :, f, :],
-                in_=ident[:].rearrange(halves, f=2, j=HALF)[:, :, 1 - f, :],
-            )
+
+        def make_partner():
+            halves = "p (h f j) -> p h f j"
+            for f in range(2):
+                nc.scalar.copy(
+                    out=partner[:].rearrange(halves, f=2, j=HALF)[:, :, f, :],
+                    in_=ident[:].rearrange(halves, f=2, j=HALF)[:, :, 1 - f, :],
+                )
 
         def make_factors(own, other, angle):
             nc.scalar.activation(out=own, in_=angle, func=SIN, bias=math.pi / 2, scale=-1.0)
@@ -292,27 +297,46 @@ def tile_attention_pa_t_kernel(tc, x, f1, f2, f3, Wqkv, out_0, out_1, out_2):
                 in_=axis0[:].rearrange("p t s (h j) -> p t (s h) j", h=HEADS),
             )
 
-        def rope_late(quantised, a, t, staged, adder):
-            ps_late = psum.tile([P, BANK], F32)
-            project(ps_late[:], quantised, a, LATE)
-            products = work.tile([P, 2, QK_HEADS, LATE_DIM], F32)
-            shape = [P, 2, QK_HEADS, LATE_DIM]
-            by_head = ps_late[:].rearrange("p (n d) -> p n d", n=QK_HEADS)
+        def late_products(ps_late, t, products, heads):
+            shape = [P, 2, heads.stop - heads.start, LATE_DIM]
+            by_head = ps_late[:].rearrange("p (n d) -> p n d", n=QK_HEADS)[:, heads]
             nc.vector.tensor_tensor(
-                out=products[:],
+                out=products[:, :, heads, :],
                 in0=by_head.unsqueeze(1).to_broadcast(shape),
                 in1=late[:, t].unsqueeze(2).to_broadcast(shape),
                 op=MULT,
             )
+
+        def late_sums(adder, products, t, staged, s):
+            heads = slice(HEADS * s.start, HEADS * s.stop)
             split = "p n (a f j) -> p n a f j"
             adder.tensor_tensor(
-                out=staged[:, 0:2, :, t % GROUP, AXIS_DIM:].rearrange(
+                out=staged[:, s, :, t % GROUP, AXIS_DIM:].rearrange(
                     "p s h (a f j) -> p (s h) a f j", a=AXES - 1, f=2
                 ),
-                in0=products[:, 0].rearrange(split, a=AXES - 1, f=2),
-                in1=products[:, 1].rearrange(split, a=AXES - 1, f=2)[:, :, :, ::-1, :],
+                in0=products[:, 0, heads].rearrange(split, a=AXES - 1, f=2),
+                in1=products[:, 1, heads].rearrange(split, a=AXES - 1, f=2)[:, :, :, ::-1, :],
                 op=ADD,
             )
+
+        def project_late(quantised, a):
+            ps_late = psum.tile([P, BANK], F32)
+            project(ps_late[:], quantised, a, LATE)
+            return ps_late
+
+        def rope_late(quantised, a, t, staged):
+            ps_late = project_late(quantised, a)
+            products = work.tile([P, 2, QK_HEADS, LATE_DIM], F32)
+            late_products(ps_late, t, products, slice(0, QK_HEADS))
+            late_sums(nc.gpsimd, products, t, staged, slice(0, 2))
+
+        def rope_last(quantised, t, staged):
+            ps_late = project_late(quantised, 1)
+            products = work.tile([P, 2, QK_HEADS, LATE_DIM], F32)
+            for s in range(2):
+                late_products(ps_late, t, products, slice(HEADS * s, HEADS * (s + 1)))
+            for s in range(2):
+                late_sums(nc.vector, products, t, staged, slice(s, s + 1))
 
         def collect_v(quantised, a, slot, staged):
             ps_v = psum.tile([P, BANK], F32)
@@ -327,22 +351,26 @@ def tile_attention_pa_t_kernel(tc, x, f1, f2, f3, Wqkv, out_0, out_1, out_2):
 
         def store(b, t0, count, staged):
             slot0 = t0 % GROUP
-            for s in (2, 0, 1):
+            for s in (0, 2, 1):
                 by_partition = outs[s][b].rearrange("h (p t) d -> p h t d", t=TILES)
                 nc.sync.dma_start(
                     out=by_partition[:, :, t0 : t0 + count, :],
                     in_=staged[:, s, :, slot0 : slot0 + count, :],
                 )
 
+        grouped_0 = transpose_pair(0)
         for g in range(PASSES):
             regroup_qk(nc.scalar.copy, g, AXIS0, 0, AXIS_DIM)
-            regroup_qk(nc.vector.tensor_copy, g, LATE, AXIS_DIM, LATE_DIM)
-            quantise_w(g, LATE)
-            quantise_w(g, AXIS0)
-        quantised = quantise_pair(transpose_pair(0))
-        make_token_factors(0)
+        regroup_qk(nc.vector.tensor_copy, 0, LATE, AXIS_DIM, LATE_DIM)
+        quantised = quantise_pair(grouped_0)
+        quantise_w(0, AXIS0)
+        regroup_qk(nc.vector.tensor_copy, 1, LATE, AXIS_DIM, LATE_DIM)
+        quantise_w(1, AXIS0)
         for g in range(PASSES):
-            regroup_v(g)
+            quantise_w(g, LATE)
+        make_token_factors(0)
+        nc.scalar.copy(out=ident_bf[:], in_=ident[:])
+        regroup_v(0)
 
         before = None
         grouped = {}
@@ -350,7 +378,7 @@ def tile_attention_pa_t_kernel(tc, x, f1, f2, f3, Wqkv, out_0, out_1, out_2):
             b, t0 = divmod(i * PAIR, TILES)
             group, slot0 = divmod(t0, GROUP)
             even_pair = slot0 == 0
-            if i + 3 < PAIRS and (i + 3) * PAIR >= TILES:
+            if SORTED_FROM <= i + 3 < PAIRS:
                 sort_words(i + 3)
             if even_pair:
                 staged = work.tile([P, 3, HEADS, GROUP, HEAD_DIM], F32)
@@ -360,20 +388,23 @@ def tile_attention_pa_t_kernel(tc, x, f1, f2, f3, Wqkv, out_0, out_1, out_2):
                 odd_products = products_odd(quantised, group)
                 if b == 0 and group + 1 < GROUPS:
                     make_token_factors(group + 1)
-            rope_late(quantised, 0, t0, staged, nc.gpsimd)
+            rope_late(quantised, 0, t0, staged)
             if i == 0:
                 grouped[1] = transpose_pair(1)
+                make_channel_factors(group, spread)
+                regroup_v(1)
             else:
                 collect_v(before[0], 0, before[2], before[1])
-                coming = quantise_pair(grouped[i + 1]) if i + 1 < PAIRS else None
+            coming = quantise_pair(grouped[i + 1]) if i + 1 < PAIRS else None
             if i > 0 and i + 2 < PAIRS:
                 grouped[i + 2] = transpose_pair(i + 2)
-            rope_late(
-                quantised, 1, t0 + 1, staged, nc.gpsimd if i + 1 < PAIRS else nc.vector
-            )
+            if i + 1 < PAIRS:
+                rope_late(quantised, 1, t0 + 1, staged)
+            else:
+                rope_last(quantised, t0 + 1, staged)
             if i == 0:
-                coming = quantise_pair(grouped[1])
                 grouped[2] = transpose_pair(2)
+                make_partner()
                 for g in range(PASSES):
                     for cols in V_PARTS:
                         quantise_w(g, cols)
@@ -381,7 +412,7 @@ def tile_attention_pa_t_kernel(tc, x, f1, f2, f3, Wqkv, out_0, out_1, out_2):
                 collect_v(before[0], 1, before[2] + 1, before[1])
             if not even_pair:
                 collect_odd(add_odd(odd_products), staged)
-            if even_pair and b == 0:
+            if even_pair and b == 0 and i > 0:
                 make_channel_factors(group, spread)
             if even_pair and i > 0:
                 last_b, last_t = divmod((i - 2) * PAIR, TILES)

@@ -40,7 +40,8 @@ PAIR = 2
 PAIRS = BATCH * TILES // PAIR
 GROUP = 4
 GROUPS = TILES // GROUP
-SORTED_FROM = 5
+SORTED_FROM = TILES // PAIR
+STORED_BY_PAIRS_FROM = PAIRS - 3
 
 FLOPS = 2 * BATCH * TOKENS * DIM * COLS
 
@@ -261,19 +262,29 @@ def tile_attention_pa_t_kernel(tc, x, f1, f2, f3, Wqkv, out_0, out_1, out_2):
                 op=ADD,
             )
 
-        def products_odd(quantised, group):
+        def products_odd(quantised, group, share):
             axis0 = psum.tile([P, 2, PAIR * P], F32)
             for s in range(2):
                 project_turned(axis0[:, s, :], quantised, slice(P * s, P * (s + 1)))
             axis0_products = work.tile([P, 2, 2, PAIR * P], F32)
-            shape = [P, 2, 2, PAIR * P]
+            mine = 1 if share else 2
+            shape = [P, 2, mine, PAIR * P]
             factors = odd[:, :, group].rearrange("p c t r -> p c (t r)")
             nc.vector.tensor_tensor(
-                out=axis0_products[:],
-                in0=axis0[:].unsqueeze(1).to_broadcast(shape),
+                out=axis0_products[:, :, :mine, :],
+                in0=axis0[:, :mine, :].unsqueeze(1).to_broadcast(shape),
                 in1=factors.unsqueeze(2).to_broadcast(shape),
                 op=MULT,
             )
+            if share:
+                turned_k = work.tile([P, PAIR * P], F32)
+                nc.scalar.copy(out=turned_k[:], in_=axis0[:, 1, :])
+                nc.gpsimd.tensor_tensor(
+                    out=axis0_products[:, :, 1, :],
+                    in0=turned_k[:].unsqueeze(1).to_broadcast([P, 2, PAIR * P]),
+                    in1=factors,
+                    op=MULT,
+                )
             return axis0_products
 
         def add_odd(axis0_products):
@@ -351,7 +362,7 @@ def tile_attention_pa_t_kernel(tc, x, f1, f2, f3, Wqkv, out_0, out_1, out_2):
 
         def store(b, t0, count, staged):
             slot0 = t0 % GROUP
-            for s in (0, 2, 1):
+            for s in (2, 0, 1):
                 by_partition = outs[s][b].rearrange("h (p t) d -> p h t d", t=TILES)
                 nc.sync.dma_start(
                     out=by_partition[:, :, t0 : t0 + count, :],
@@ -372,35 +383,50 @@ def tile_attention_pa_t_kernel(tc, x, f1, f2, f3, Wqkv, out_0, out_1, out_2):
         nc.scalar.copy(out=ident_bf[:], in_=ident[:])
         regroup_v(0)
 
-        before = None
+        waiting_v = []
+
+        def collect_waiting(count):
+            for _ in range(count):
+                collect_v(*waiting_v.pop(0))
+
         grouped = {}
         for i in range(PAIRS):
             b, t0 = divmod(i * PAIR, TILES)
             group, slot0 = divmod(t0, GROUP)
             even_pair = slot0 == 0
+            next_group = group + 1 if b == 0 and group + 1 < GROUPS else None
             if SORTED_FROM <= i + 3 < PAIRS:
                 sort_words(i + 3)
             if even_pair:
+                last_staged = staged if i > 0 else None
                 staged = work.tile([P, 3, HEADS, GROUP, HEAD_DIM], F32)
                 rope_even(quantised, group, staged)
                 spread = spread_angles(group) if b == 0 else None
             else:
-                odd_products = products_odd(quantised, group)
-                if b == 0 and group + 1 < GROUPS:
-                    make_token_factors(group + 1)
+                odd_products = products_odd(quantised, group, share=i + 1 < PAIRS)
+                if next_group is not None:
+                    make_token_factors(next_group)
             rope_late(quantised, 0, t0, staged)
             if i == 0:
                 grouped[1] = transpose_pair(1)
-                make_channel_factors(group, spread)
+                make_channel_factors(0, spread)
                 regroup_v(1)
+            elif i + 1 < PAIRS:
+                collect_waiting(1)
             else:
-                collect_v(before[0], 0, before[2], before[1])
+                collect_waiting(len(waiting_v))
             coming = quantise_pair(grouped[i + 1]) if i + 1 < PAIRS else None
+            turned_back = add_odd(odd_products) if even_pair and i > 0 else None
             if i > 0 and i + 2 < PAIRS:
                 grouped[i + 2] = transpose_pair(i + 2)
+            if turned_back is not None:
+                collect_odd(turned_back, last_staged)
+            for a in range(PAIR):
+                waiting_v.append((quantised, a, slot0 + a, staged))
             if i + 1 < PAIRS:
                 rope_late(quantised, 1, t0 + 1, staged)
             else:
+                collect_waiting(1)
                 rope_last(quantised, t0 + 1, staged)
             if i == 0:
                 grouped[2] = transpose_pair(2)
@@ -409,17 +435,15 @@ def tile_attention_pa_t_kernel(tc, x, f1, f2, f3, Wqkv, out_0, out_1, out_2):
                     for cols in V_PARTS:
                         quantise_w(g, cols)
             else:
-                collect_v(before[0], 1, before[2] + 1, before[1])
-            if not even_pair:
-                collect_odd(add_odd(odd_products), staged)
+                collect_waiting(1 if i + 2 < PAIRS else len(waiting_v))
             if even_pair and b == 0 and i > 0:
                 make_channel_factors(group, spread)
-            if even_pair and i > 0:
+            if i >= STORED_BY_PAIRS_FROM:
+                last_b, last_t = divmod((i - 1) * PAIR, TILES)
+                store(last_b, last_t, PAIR, last_staged if even_pair else staged)
+            elif even_pair and i > 0:
                 last_b, last_t = divmod((i - 2) * PAIR, TILES)
-                store(last_b, last_t, GROUP, before[1])
-            before = (quantised, staged, slot0)
+                store(last_b, last_t, GROUP, last_staged)
             quantised = coming
-        store(BATCH - 1, TILES - GROUP, PAIR, staged)
-        for a in range(PAIR):
-            collect_v(before[0], a, PAIR + a, staged)
+        collect_odd(add_odd(odd_products), staged)
         store(BATCH - 1, TILES - PAIR, PAIR, staged)

@@ -40,7 +40,7 @@ PAIR = 2
 PAIRS = BATCH * TILES // PAIR
 GROUP = 4
 GROUPS = TILES // GROUP
-SORTED_FROM = TILES // PAIR
+SORTED_FROM = 5
 STORED_BY_PAIRS_FROM = PAIRS - 3
 
 FLOPS = 2 * BATCH * TOKENS * DIM * COLS
@@ -262,29 +262,19 @@ def tile_attention_pa_t_kernel(tc, x, f1, f2, f3, Wqkv, out_0, out_1, out_2):
                 op=ADD,
             )
 
-        def products_odd(quantised, group, share):
+        def products_odd(quantised, group):
             axis0 = psum.tile([P, 2, PAIR * P], F32)
             for s in range(2):
                 project_turned(axis0[:, s, :], quantised, slice(P * s, P * (s + 1)))
             axis0_products = work.tile([P, 2, 2, PAIR * P], F32)
-            mine = 1 if share else 2
-            shape = [P, 2, mine, PAIR * P]
+            shape = [P, 2, 2, PAIR * P]
             factors = odd[:, :, group].rearrange("p c t r -> p c (t r)")
             nc.vector.tensor_tensor(
-                out=axis0_products[:, :, :mine, :],
-                in0=axis0[:, :mine, :].unsqueeze(1).to_broadcast(shape),
+                out=axis0_products[:],
+                in0=axis0[:].unsqueeze(1).to_broadcast(shape),
                 in1=factors.unsqueeze(2).to_broadcast(shape),
                 op=MULT,
             )
-            if share:
-                turned_k = work.tile([P, PAIR * P], F32)
-                nc.scalar.copy(out=turned_k[:], in_=axis0[:, 1, :])
-                nc.gpsimd.tensor_tensor(
-                    out=axis0_products[:, :, 1, :],
-                    in0=turned_k[:].unsqueeze(1).to_broadcast([P, 2, PAIR * P]),
-                    in1=factors,
-                    op=MULT,
-                )
             return axis0_products
 
         def add_odd(axis0_products):
@@ -397,13 +387,14 @@ def tile_attention_pa_t_kernel(tc, x, f1, f2, f3, Wqkv, out_0, out_1, out_2):
             next_group = group + 1 if b == 0 and group + 1 < GROUPS else None
             if SORTED_FROM <= i + 3 < PAIRS:
                 sort_words(i + 3)
+            coming = quantise_pair(grouped[i + 1]) if even_pair and i > 0 else None
             if even_pair:
                 last_staged = staged if i > 0 else None
                 staged = work.tile([P, 3, HEADS, GROUP, HEAD_DIM], F32)
                 rope_even(quantised, group, staged)
                 spread = spread_angles(group) if b == 0 else None
             else:
-                odd_products = products_odd(quantised, group, share=i + 1 < PAIRS)
+                odd_products = products_odd(quantised, group)
                 if next_group is not None:
                     make_token_factors(next_group)
             rope_late(quantised, 0, t0, staged)
@@ -415,12 +406,10 @@ def tile_attention_pa_t_kernel(tc, x, f1, f2, f3, Wqkv, out_0, out_1, out_2):
                 collect_waiting(1)
             else:
                 collect_waiting(len(waiting_v))
-            coming = quantise_pair(grouped[i + 1]) if i + 1 < PAIRS else None
-            turned_back = add_odd(odd_products) if even_pair and i > 0 else None
+            if coming is None and i + 1 < PAIRS:
+                coming = quantise_pair(grouped[i + 1])
             if i > 0 and i + 2 < PAIRS:
                 grouped[i + 2] = transpose_pair(i + 2)
-            if turned_back is not None:
-                collect_odd(turned_back, last_staged)
             for a in range(PAIR):
                 waiting_v.append((quantised, a, slot0 + a, staged))
             if i + 1 < PAIRS:
@@ -436,6 +425,8 @@ def tile_attention_pa_t_kernel(tc, x, f1, f2, f3, Wqkv, out_0, out_1, out_2):
                         quantise_w(g, cols)
             else:
                 collect_waiting(1 if i + 2 < PAIRS else len(waiting_v))
+            if not even_pair:
+                collect_odd(add_odd(odd_products), staged)
             if even_pair and b == 0 and i > 0:
                 make_channel_factors(group, spread)
             if i >= STORED_BY_PAIRS_FROM:
@@ -445,5 +436,4 @@ def tile_attention_pa_t_kernel(tc, x, f1, f2, f3, Wqkv, out_0, out_1, out_2):
                 last_b, last_t = divmod((i - 2) * PAIR, TILES)
                 store(last_b, last_t, GROUP, last_staged)
             quantised = coming
-        collect_odd(add_odd(odd_products), staged)
         store(BATCH - 1, TILES - PAIR, PAIR, staged)

import math
from contextlib import ExitStack

import concourse.mybir as mybir
from concourse.masks import make_identity

F32 = mybir.dt.float32
BF16 = mybir.dt.bfloat16
U32 = mybir.dt.uint32
U8 = mybir.dt.uint8
FP8X4 = mybir.dt.float8_e4m3fn_x4
MULT = mybir.AluOpType.mult
ADD = mybir.AluOpType.add
SIN = mybir.ActivationFunctionType.Sin

BATCH = 2
TOKENS = 2048
DIM = 1024
HEADS = 4
HEAD_DIM = 96
AXES = 3
AXIS_DIM = HEAD_DIM // AXES
HALF = AXIS_DIM // 2
LATE_DIM = HEAD_DIM - AXIS_DIM
QK_HEADS = 2 * HEADS

P = 128
PACK = 4
K_PASS = P * PACK
PASSES = DIM // K_PASS
BLOCK = HEADS * HEAD_DIM
COLS = 3 * BLOCK
AXIS0 = slice(0, QK_HEADS * AXIS_DIM)
LATE = slice(AXIS0.stop, AXIS0.stop + QK_HEADS * LATE_DIM)
V_PARTS = (slice(768, 1024), slice(1024, 1152))
BANK = 512

TILES = TOKENS // P
PAIR = 2
PAIRS = BATCH * TILES // PAIR
GROUP = 4
GROUPS = TILES // GROUP
SORTED_FROM = 5
STORED_BY_PAIRS_FROM = PAIRS - 3

FLOPS = 2 * BATCH * TOKENS * DIM * COLS


def tile_attention_pa_t_kernel(tc, x, f1, f2, f3, Wqkv, out_0, out_1, out_2):
    nc = tc.nc
    outs = (out_0, out_1, out_2)

    with ExitStack() as ctx:
        const = ctx.enter_context(tc.tile_pool(name="const", bufs=1))
        x_pool = ctx.enter_context(tc.tile_pool(name="x", bufs=12))
        work = ctx.enter_context(tc.tile_pool(name="work", bufs=3))
        psum = ctx.enter_context(tc.psum_pool(name="psum", bufs=2))
        ctx.enter_context(tc.manual_schedule())

        def load_x_pair(i):
            b, t = divmod(i * PAIR, TILES)
            x_pair = x_pool.tile([P, PAIR, DIM], BF16)
            by_partition = x[b].rearrange("(p t) k -> p t k", t=TILES)
            nc.sync.dma_start(out=x_pair[:], in_=by_partition[:, t : t + PAIR, :])
            return x_pair

        def load_w(g, cols):
            w_rows = const.tile([P, PACK, cols.stop - cols.start], BF16, name="w%d_%d" % (g, cols.start))
            by_partition = Wqkv[K_PASS * g : K_PASS * (g + 1), :].rearrange(
                "(p t) c -> p t c", t=PACK
            )
            nc.sync.dma_start(out=w_rows[:], in_=by_partition[:, :, cols])
            return w_rows

        x_pairs = [load_x_pair(0)]
        qk_rows = [load_w(g, slice(0, 2 * BLOCK)) for g in range(PASSES)]
        angles = const.tile([P, AXES, TILES, AXIS_DIM], BF16)
        for axis, f in enumerate((f1, f2, f3)):
            nc.sync.dma_start(out=angles[:, axis], in_=f.rearrange("(p t) j -> p t j", t=TILES))
        v_rows = []
        for g in range(PASSES):
            v_rows.append(load_w(g, slice(2 * BLOCK, COLS)))
            x_pairs.append(load_x_pair(1 + g))
        for i in range(1 + PASSES, PAIRS):
            x_pairs.append(load_x_pair(i))

        warm = const.tile([P, 1], F32)
        nc.vector.memset(warm[:], 0.0)
        nc.scalar.activation(out=warm[:], in_=warm[:], func=SIN)

        ident = const.tile([P, P], F32)
        make_identity(nc, ident[:])
        ident_bf = const.tile([P, P], BF16)
        partner = const.tile([P, P], F32)

        def make_partner():
            halves = "p (h f j) -> p h f j"
            for f in range(2):
                nc.scalar.copy(
                    out=partner[:].rearrange(halves, f=2, j=HALF)[:, :, f, :],
                    in_=ident[:].rearrange(halves, f=2, j=HALF)[:, :, 1 - f, :],
                )

        def make_factors(own, other, angle):
            nc.scalar.activation(out=own, in_=angle, func=SIN, bias=math.pi / 2, scale=-1.0)
            nc.scalar.activation(out=other[:, :, :, :HALF], in_=angle[:, :, :, HALF:], func=SIN)
            nc.scalar.activation(
                out=other[:, :, :, HALF:], in_=angle[:, :, :, :HALF], func=SIN, scale=-1.0
            )

        late = const.tile([P, TILES, 2, LATE_DIM], F32)
        even = const.tile([P, GROUPS, 2, PAIR, AXIS_DIM], F32)
        odd = const.tile([P, 2, GROUPS, PAIR, P], F32)

        def make_token_factors(group):
            tiles = slice(GROUP * group, GROUP * (group + 1))
            by_axis = "p t (a j) -> p t a j"
            make_factors(
                late[:, tiles, 0, :].rearrange(by_axis, a=AXES - 1),
                late[:, tiles, 1, :].rearrange(by_axis, a=AXES - 1),
                angles[:, 1:, tiles, :].rearrange("p a t j -> p t a j"),
            )
            pair = slice(GROUP * group, GROUP * group + PAIR)
            make_factors(
                even[:, group, 0].unsqueeze(1),
                even[:, group, 1].unsqueeze(1),
                angles[:, 0, pair, :].unsqueeze(1),
            )

        def spread_angles(group):
            spread = work.tile([P, 2, PAIR, HEADS, AXIS_DIM], BF16)
            tiles = slice(GROUP * group + PAIR, GROUP * (group + 1))
            angle = angles[:, 0, tiles, :].unsqueeze(2).to_broadcast([P, PAIR, HEADS, AXIS_DIM])
            nc.scalar.copy(out=spread[:, 0], in_=angle)
            nc.scalar.copy(out=spread[:, 1, :, :, :HALF], in_=angle[:, :, :, HALF:])
            nc.scalar.mul(spread[:, 1, :, :, HALF:], angle[:, :, :, :HALF], -1.0)
            return spread

        def make_channel_factors(group, spread):
            xt = psum.tile([P, 2, PAIR, P], BF16)
            for c in range(2):
                for a in range(PAIR):
                    nc.tensor.transpose(
                        xt[:, c, a, :], spread[:, c, a].rearrange("p h j -> p (h j)"), ident_bf[:]
                    )
            nc.scalar.activation(
                out=odd[:, 0, group], in_=xt[:, 0], func=SIN, bias=math.pi / 2, scale=-1.0
            )
            nc.scalar.activation(out=odd[:, 1, group], in_=xt[:, 1], func=SIN)

        sorted_words = {}

        def words_in_place(i):
            return x_pairs[i][:].bitcast(F32).rearrange("p a (g w u) -> p a g u w", g=PASSES, u=2)

        def sort_words(i):
            words = work.tile([P, PAIR, PASSES, 2, P], F32)
            nc.scalar.copy(out=words[:], in_=words_in_place(i))
            sorted_words[i] = words

        def transpose_pair(i):
            words = sorted_words[i] if i in sorted_words else words_in_place(i)
            grouped = work.tile([P, PASSES, PAIR, P, PACK], BF16, align_bytes=64)
            for a in range(PAIR):
                xt = psum.tile([P, PASSES * 2, P], F32)
                for g in range(PASSES):
                    for u in range(2):
                        nc.tensor.transpose(xt[:, 2 * g + u, :], words[:, a, g, u, :], ident[:])
                nc.scalar.copy(
                    out=grouped[:, :, a].bitcast(F32),
                    in_=xt[:].rearrange("p (g u) r -> p g r u", u=2),
                )
            return grouped

        def quantise_pair(grouped):
            x_codes = work.tile([P, PASSES, PAIR, P], U32, align_bytes=64)
            x_scales = work.tile([P, PASSES, PAIR, P], U8, align_bytes=64)
            nc.vector.quantize_mx(
                out=x_codes[:].rearrange("p g a r -> p (g a r)").bitcast(FP8X4),
                scales=x_scales[:].rearrange("p g a r -> p (g a r)"),
                in_=grouped[:].rearrange("p g a r t -> p (g a r t)"),
            )
            return x_codes, x_scales

        w_grouped = const.tile([P, PASSES, COLS, PACK], BF16, align_bytes=64)
        w_codes = const.tile([P, PASSES, COLS], U32, align_bytes=64)
        w_scales = const.tile([P, PASSES, COLS], U8, align_bytes=64)

        def regroup_qk(copy, g, cols, d0, width):
            rows = qk_rows[g][:].rearrange("p t (n d) -> p n t d", d=HEAD_DIM)
            copy(
                out=w_grouped[:, g, cols, :].rearrange(
                    "p (n c i) t -> p n c t i", n=QK_HEADS, i=4
                ),
                in_=rows[:, :, :, d0 : d0 + width].rearrange("p n t (c i) -> p n c t i", i=4),
            )

        def regroup_v(g):
            nc.scalar.copy(
                out=w_grouped[:, g, 2 * BLOCK :, :].rearrange("p (c i) t -> p c t i", i=4),
                in_=v_rows[g][:].rearrange("p t (c i) -> p c t i", i=4),
            )

        def quantise_w(g, cols):
            nc.vector.quantize_mx(
                out=w_codes[:, g, cols].bitcast(FP8X4),
                scales=w_scales[:, g, cols],
                in_=w_grouped[:, g, cols, :].rearrange("p c t -> p (c t)"),
            )

        def multiply(out, lhsT, lhsT_scale, rhs, rhs_scale):
            for g in range(PASSES):
                nc.tensor.matmul_mx(
                    out=out,
                    lhsT=lhsT(g).bitcast(FP8X4),
                    lhsT_scale=lhsT_scale(g),
                    rhs=rhs(g).bitcast(FP8X4),
                    rhs_scale=rhs_scale(g),
                    start=(g == 0),
                    stop=(g == PASSES - 1),
                )

        def project(out, quantised, a, cols):
            x_codes, x_scales = quantised
            multiply(
                out,
                lambda g: x_codes[:, g, a, :],
                lambda g: x_scales[:, g, a, :],
                lambda g: w_codes[:, g, cols],
                lambda g: w_scales[:, g, cols],
            )

        def project_turned(out, quantised, cols):
            x_codes, x_scales = quantised
            multiply(
                out,
                lambda g: w_codes[:, g, cols],
                lambda g: w_scales[:, g, cols],
                lambda g: x_codes[:, g].rearrange("p a r -> p (a r)"),
                lambda g: x_scales[:, g].rearrange("p a r -> p (a r)"),
            )

        def rope_even(quantised, group, staged):
            axis0 = psum.tile([P, PAIR, QK_HEADS, AXIS_DIM], F32)
            for a in range(PAIR):
                project(axis0[:, a].rearrange("p n j -> p (n j)"), quantised, a, AXIS0)
            axis0_products = work.tile([P, 2, PAIR, QK_HEADS, AXIS_DIM], F32)
            shape = [P, 2, PAIR, QK_HEADS, AXIS_DIM]
            nc.vector.tensor_tensor(
                out=axis0_products[:],
                in0=axis0[:].unsqueeze(1).to_broadcast(shape),
                in1=even[:, group].unsqueeze(3).to_broadcast(shape),
                op=MULT,
            )
            halved = "p t n (f j) -> p t n f j"
            nc.gpsimd.tensor_tensor(
                out=staged[:, 0:2, :, :PAIR, :AXIS_DIM].rearrange(
                    "p s h t (f j) -> p t (s h) f j", f=2
                ),
                in0=axis0_products[:, 0].rearrange(halved, f=2),
                in1=axis0_products[:, 1].rearrange(halved, f=2)[:, :, :, ::-1, :],
                op=ADD,
            )

        def products_odd(quantised, group):
            axis0 = psum.tile([P, 2, PAIR * P], F32)
            for s in range(2):
                project_turned(axis0[:, s, :], quantised, slice(P * s, P * (s + 1)))
            axis0_products = work.tile([P, 2, 2, PAIR * P], F32)
            shape = [P, 2, 2, PAIR * P]
            factors = odd[:, :, group].rearrange("p c t r -> p c (t r)")
            nc.vector.tensor_tensor(
                out=axis0_products[:],
                in0=axis0[:].unsqueeze(1).to_broadcast(shape),
                in1=factors.unsqueeze(2).to_broadcast(shape),
                op=MULT,
            )
            return axis0_products

        def add_odd(axis0_products):
            axis0 = psum.tile([P, PAIR, 2, P], F32)
            for a in range(PAIR):
                for s in range(2):
                    for c, order in enumerate((ident, partner)):
                        nc.tensor.matmul(
                            axis0[:, a, s, :],
                            lhsT=axis0_products[:, c, s, P * a : P * (a + 1)],
                            rhs=order[:],
                            start=(c == 0),
                            stop=(c == 1),
                            is_transpose=True,
                        )
            return axis0

        def collect_odd(axis0, staged):
            nc.scalar.copy(
                out=staged[:, 0:2, :, PAIR:, :AXIS_DIM].rearrange("p s h t j -> p t (s h) j"),
                in_=axis0[:].rearrange("p t s (h j) -> p t (s h) j", h=HEADS),
            )

        def late_products(ps_late, t, products, heads):
            shape = [P, 2, heads.stop - heads.start, LATE_DIM]
            by_head = ps_late[:].rearrange("p (n d) -> p n d", n=QK_HEADS)[:, heads]
            nc.vector.tensor_tensor(
                out=products[:, :, heads, :],
                in0=by_head.unsqueeze(1).to_broadcast(shape),
                in1=late[:, t].unsqueeze(2).to_broadcast(shape),
                op=MULT,
            )

        def late_sums(adder, products, t, staged, s):
            heads = slice(HEADS * s.start, HEADS * s.stop)
            split = "p n (a f j) -> p n a f j"
            adder.tensor_tensor(
                out=staged[:, s, :, t % GROUP, AXIS_DIM:].rearrange(
                    "p s h (a f j) -> p (s h) a f j", a=AXES - 1, f=2
                ),
                in0=products[:, 0, heads].rearrange(split, a=AXES - 1, f=2),
                in1=products[:, 1, heads].rearrange(split, a=AXES - 1, f=2)[:, :, :, ::-1, :],
                op=ADD,
            )

        def project_late(quantised, a):
            ps_late = psum.tile([P, BANK], F32)
            project(ps_late[:], quantised, a, LATE)
            return ps_late

        def rope_late(quantised, a, t, staged):
            ps_late = project_late(quantised, a)
            products = work.tile([P, 2, QK_HEADS, LATE_DIM], F32)
            late_products(ps_late, t, products, slice(0, QK_HEADS))
            late_sums(nc.gpsimd, products, t, staged, slice(0, 2))

        def rope_last(quantised, t, staged):
            ps_late = project_late(quantised, 1)
            products = work.tile([P, 2, QK_HEADS, LATE_DIM], F32)
            for s in range(2):
                late_products(ps_late, t, products, slice(HEADS * s, HEADS * (s + 1)))
            for s in range(2):
                late_sums(nc.vector, products, t, staged, slice(s, s + 1))

        def collect_v(quantised, a, slot, staged):
            ps_v = psum.tile([P, BANK], F32)
            for cols in V_PARTS:
                project(
                    ps_v[:, cols.start - 2 * BLOCK : cols.stop - 2 * BLOCK], quantised, a, cols
                )
            nc.scalar.copy(
                out=staged[:, 2, :, slot, :],
                in_=ps_v[:, :BLOCK].rearrange("p (h d) -> p h d", h=HEADS),
            )

        def store(b, t0, count, staged):
            slot0 = t0 % GROUP
            for s in (2, 0, 1):
                by_partition = outs[s][b].rearrange("h (p t) d -> p h t d", t=TILES)
                nc.sync.dma_start(
                    out=by_partition[:, :, t0 : t0 + count, :],
                    in_=staged[:, s, :, slot0 : slot0 + count, :],
                )

        grouped_0 = transpose_pair(0)
        for g in range(PASSES):
            regroup_qk(nc.scalar.copy, g, AXIS0, 0, AXIS_DIM)
        regroup_qk(nc.vector.tensor_copy, 0, LATE, AXIS_DIM, LATE_DIM)
        quantised = quantise_pair(grouped_0)
        quantise_w(0, AXIS0)
        regroup_qk(nc.vector.tensor_copy, 1, LATE, AXIS_DIM, LATE_DIM)
        quantise_w(1, AXIS0)
        for g in range(PASSES):
            quantise_w(g, LATE)
        make_token_factors(0)
        nc.scalar.copy(out=ident_bf[:], in_=ident[:])
        regroup_v(0)

        waiting_v = []

        def collect_waiting(count):
            for _ in range(count):
                collect_v(*waiting_v.pop(0))

        grouped = {}
        for i in range(PAIRS):
            b, t0 = divmod(i * PAIR, TILES)
            group, slot0 = divmod(t0, GROUP)
            even_pair = slot0 == 0
            next_group = group + 1 if b == 0 and group + 1 < GROUPS else None
            if SORTED_FROM <= i + 3 < PAIRS:
                sort_words(i + 3)
            coming = quantise_pair(grouped[i + 1]) if even_pair and i > 0 else None
            if even_pair:
                last_staged = staged if i > 0 else None
                staged = work.tile([P, 3, HEADS, GROUP, HEAD_DIM], F32)
                rope_even(quantised, group, staged)
                spread = spread_angles(group) if b == 0 else None
            else:
                odd_products = products_odd(quantised, group)
                if next_group is not None:
                    make_token_factors(next_group)
            rope_late(quantised, 0, t0, staged)
            if i == 0:
                grouped[1] = transpose_pair(1)
                make_channel_factors(0, spread)
                regroup_v(1)
            elif i + 1 < PAIRS:
                collect_waiting(1)
            else:
                collect_waiting(len(waiting_v))
            if coming is None and i + 1 < PAIRS:
                coming = quantise_pair(grouped[i + 1])
            if i > 0 and i + 2 < PAIRS:
                grouped[i + 2] = transpose_pair(i + 2)
            for a in range(PAIR):
                waiting_v.append((quantised, a, slot0 + a, staged))
            if i + 1 < PAIRS:
                rope_late(quantised, 1, t0 + 1, staged)
            else:
                collect_waiting(1)
                rope_last(quantised, t0 + 1, staged)
            if i == 0:
                grouped[2] = transpose_pair(2)
                make_partner()
                for g in range(PASSES):
                    for cols in V_PARTS:
                        quantise_w(g, cols)
            else:
                collect_waiting(1 if i + 2 < PAIRS else len(waiting_v))
            if not even_pair:
                collect_odd(add_odd(odd_products), staged)
            if even_pair and b == 0 and i > 0:
                make_channel_factors(group, spread)
            if i >= STORED_BY_PAIRS_FROM:
                last_b, last_t = divmod((i - 1) * PAIR, TILES)
                store(last_b, last_t, PAIR, last_staged if even_pair else staged)
            elif even_pair and i > 0:
                last_b, last_t = divmod((i - 2) * PAIR, TILES)
                store(last_b, last_t, GROUP, last_staged)
            quantised = coming
        store(BATCH - 1, TILES - PAIR, PAIR, staged)
